import numpy as np
import ml_dtypes


def mxq(x, axis, fmt="e4m3"):
    dtype, down = {"e4m3": (ml_dtypes.float8_e4m3fn, 7), "e5m2": (ml_dtypes.float8_e5m2, 14)}[fmt]
    v = np.moveaxis(np.asarray(x, np.float32).astype(ml_dtypes.bfloat16).astype(np.float64), axis, -1)
    blocks = v.reshape(v.shape[:-1] + (-1, 32))
    amax = np.abs(blocks).max(-1, keepdims=True)
    byte = np.maximum(np.where(amax > 0, np.frexp(amax)[1] - 1 + 127, 0) - down, 1)
    scale = np.exp2(byte - 127.0)
    codes = (blocks / scale).astype(np.float32).astype(dtype).astype(np.float64)
    return np.moveaxis((codes * scale).reshape(v.shape), -1, axis)


WIDE = False


def mx_kscale(k):
    if not WIDE:
        return np.ones(k)
    levels = np.array([10, -10, 5, -5, 0])
    if k % 512:
        return np.exp2(np.random.permutation(np.resize(levels, k // 32))).repeat(32)
    a = np.empty((k // 512, 16))
    for p in range(k // 512):
        a[p, :8] = np.random.permutation(np.resize(levels, 8))
        for g in range(8):
            far = levels[np.abs(levels - a[p, g]) >= 10]
            a[p, g + 8] = far[np.random.randint(len(far))]
    return np.exp2(a.ravel()).repeat(32)


BF16 = ml_dtypes.bfloat16


def bf(x):
    return np.asarray(x, np.float32).astype(BF16)


def f64(x):
    return np.asarray(x).astype(np.float64)


B, T, D, H, DK, ROPE, NOPE, VD, KVR, QR = 1, 1024, 2048, 16, 128, 64, 64, 128, 512, 1024
EPS = 1.1920928955078125e-07
HALF = ROPE // 2


def rms_norm(h, w):
    var = np.mean(h * h, axis=-1, keepdims=True)
    return h * (1.0 / np.sqrt(var + EPS)) * w


def rope(v):
    inv_freq = 1.0 / (10000.0 ** (f64(np.arange(0, ROPE, 2)) / ROPE))
    freqs = np.outer(f64(np.arange(v.shape[-2])), inv_freq)
    cos, sin = np.cos(freqs), np.sin(freqs)
    v1, v2 = v[..., :HALF], v[..., HALF:]
    return np.concatenate([v1 * cos - v2 * sin, v1 * sin + v2 * cos], axis=-1)


def setup_inputs():
    s, t = mx_kscale(D), mx_kscale(KVR)
    return {'x': bf(np.random.standard_normal((B, T, D)) * s),
            'wkv_c': bf(np.random.standard_normal((D, KVR)) / np.sqrt(D) / s[:, None]),
            'kv_a_norm_w': bf((1.0 + 0.1 * np.random.standard_normal(KVR)) * t),
            'wkv_b': bf(np.random.standard_normal((KVR, H * (NOPE + VD))) / np.sqrt(KVR) / t[:, None]),
            'k_pe': bf(np.random.standard_normal((B, T, ROPE)))}


def reference(x, wkv_c, kv_a_norm_w, wkv_b, k_pe):
    c = mxq(f64(x), 2, 'e4m3') @ mxq(f64(wkv_c), 0, 'e4m3')
    cn = rms_norm(c, f64(kv_a_norm_w))
    kv = mxq(cn, 2, 'e4m3') @ mxq(f64(wkv_b), 0, 'e4m3')
    kv = kv.reshape(B, T, H, NOPE + VD).transpose(0, 2, 1, 3)
    k_nope, v = kv[..., :NOPE], kv[..., NOPE:]
    k_rot = rope(f64(k_pe)[:, None])
    k_rot = np.broadcast_to(k_rot, (B, H, T, ROPE))
    ks = np.concatenate([k_nope, k_rot], axis=-1)
    return ks, np.ascontiguousarray(v)

@@ -1,0 +1,438 @@
+import math
+from contextlib import ExitStack
+
+import concourse.mybir as mybir
+from concourse.masks import make_identity
+
+F32 = mybir.dt.float32
+BF16 = mybir.dt.bfloat16
+I32 = mybir.dt.int32
+U32 = mybir.dt.uint32
+U8 = mybir.dt.uint8
+FP8X4 = mybir.dt.float8_e4m3fn_x4
+ALU = mybir.AluOpType
+ACT = mybir.ActivationFunctionType
+
+P = 128
+PACK = 4
+K_PASS = P * PACK
+RUN = 4
+
+T, D, KVR, H, NOPE, VD, ROPE = 1024, 2048, 512, 16, 64, 128, 64
+HALF_ROPE = ROPE // 2
+ROPE_BASE = 10000.0
+EPS = 2.0 ** -23
+
+TOK_TILES = T // P
+X_PASSES = D // K_PASS
+HEAD_COLS = NOPE + VD
+GROUP = 4
+GROUPS = H // GROUP
+HALVES = 2
+HALF_TILES = TOK_TILES // HALVES
+
+TWO_PI = 2.0 * math.pi
+TWO_PI_HI = 6.28125
+TWO_PI_LO = TWO_PI - TWO_PI_HI
+
+FLOPS = 2 * T * D * KVR + 2 * T * KVR * H * HEAD_COLS
+
+
+def tile_deepseekmultiheadattention_pb_kernel(
+    tc, x, wkv_c, kv_a_norm_w, wkv_b, k_pe, out_0, out_1
+):
+    nc = tc.nc
+    with ExitStack() as ctx:
+        const = ctx.enter_context(tc.tile_pool(name="const", bufs=1))
+        keep = ctx.enter_context(tc.tile_pool(name="keep", bufs=1))
+        work = ctx.enter_context(tc.tile_pool(name="work", bufs=2))
+        psum = ctx.enter_context(tc.psum_pool(name="psum", bufs=8))
+        ctx.enter_context(tc.manual_schedule())
+
+        x_view = x.rearrange("b (p i) k -> p (b i) k", i=TOK_TILES)
+        wb_view = wkv_b.rearrange("(p t) n -> p t n", t=PACK)
+        ks_view = out_0.rearrange("b h (p i) d -> p (b h) i d", i=TOK_TILES)
+        v_view = out_1.rearrange("b h (p i) d -> p (b h) i d", i=TOK_TILES)
+
+        gain_row = const.tile([P, KVR], BF16, name="gain_row")
+        nc.vector.memset(gain_row[:], 0.0)
+        nc.sync.dma_start(
+            out=gain_row[0:1, :], in_=kv_a_norm_w.rearrange("(o n) -> o n", o=1)
+        )
+        kp = const.tile([P, TOK_TILES, 2, HALF_ROPE], BF16, name="kp")
+        nc.sync.dma_start(
+            out=kp[:],
+            in_=k_pe.rearrange("b (p i) (s j) -> p (b i) s j", i=TOK_TILES, s=2),
+        )
+
+        x_pairs = [
+            keep.tile([P, 2, D], BF16, name="x_pair%d" % j) for j in range(TOK_TILES // 2)
+        ]
+        wc_raw = [
+            keep.tile([P, PACK, KVR], BF16, name="wc_raw%d" % g) for g in range(X_PASSES)
+        ]
+        wb_raw = [
+            keep.tile([P, PACK, GROUP * HEAD_COLS], BF16, name="wb_raw%d" % m)
+            for m in range(GROUPS)
+        ]
+
+        def load_x_pair(j):
+            nc.sync.dma_start(out=x_pairs[j][:], in_=x_view[:, 2 * j : 2 * j + 2, :])
+
+        def load_wb(m):
+            cols = slice(GROUP * HEAD_COLS * m, GROUP * HEAD_COLS * (m + 1))
+            nc.sync.dma_start(out=wb_raw[m][:], in_=wb_view[:, :, cols])
+
+        for g in range(X_PASSES):
+            nc.sync.dma_start(
+                out=wc_raw[g][:],
+                in_=wkv_c[K_PASS * g : K_PASS * (g + 1), :].rearrange(
+                    "(q t) c -> q t c", t=PACK
+                ),
+            )
+        load_x_pair(0)
+        load_x_pair(1)
+        load_wb(0)
+        load_x_pair(2)
+        load_x_pair(3)
+        for m in range(1, GROUPS):
+            load_wb(m)
+
+        ones = const.tile([P, P], BF16, name="ones")
+        nc.vector.memset(ones[:], 1.0)
+        table_warmer = const.tile([P, 1], F32, name="table_warmer")
+        nc.vector.memset(table_warmer[:], 1.0)
+
+        pos = const.tile([P, TOK_TILES], F32, name="pos")
+        nc.gpsimd.iota(
+            pos[:],
+            pattern=[[1, TOK_TILES]],
+            base=0,
+            channel_multiplier=TOK_TILES,
+            allow_small_or_imprecise_dtypes=True,
+        )
+        ident_f32 = const.tile([P, P], F32, name="ident_f32")
+        make_identity(nc, ident_f32[:])
+        ident_bf16 = const.tile([P, P], BF16, name="ident_bf16")
+        make_identity(nc, ident_bf16[:])
+        angle = const.tile([P, TOK_TILES, HALF_ROPE], F32, name="angle")
+        nc.vector.tensor_copy(out=angle[:, :, 0], in_=pos[:])
+        for step in range(5):
+            width = 2 ** step
+            nc.vector.tensor_scalar_mul(
+                out=angle[:, :, width : 2 * width],
+                in0=angle[:, :, 0:width],
+                scalar1=ROPE_BASE ** (-width / HALF_ROPE),
+            )
+        angle_flat = angle[:].rearrange("p i j -> p (i j)")
+        n_angles = TOK_TILES * HALF_ROPE
+        turns = const.tile([P, n_angles], I32, name="turns")
+        nc.vector.tensor_scalar(
+            out=turns[:], in0=angle_flat, scalar1=1.0 / TWO_PI, scalar2=None, op0=ALU.mult
+        )
+        coarse = const.tile([P, n_angles], F32, name="coarse")
+        nc.vector.scalar_tensor_tensor(
+            out=coarse[:], in0=turns[:], scalar=-TWO_PI_HI, in1=angle_flat,
+            op0=ALU.mult, op1=ALU.add,
+        )
+        phase = const.tile([P, 2, n_angles], F32, name="phase")
+        nc.vector.scalar_tensor_tensor(
+            out=phase[:, 0, :], in0=turns[:], scalar=-TWO_PI_LO, in1=coarse[:],
+            op0=ALU.mult, op1=ALU.add,
+        )
+        nc.vector.tensor_scalar_add(
+            out=phase[:, 1, :], in0=phase[:, 0, :], scalar1=math.pi / 2.0
+        )
+        wrap = const.tile([P, 2, n_angles], F32, name="wrap")
+        nc.vector.tensor_scalar(
+            out=wrap[:], in0=phase[:], scalar1=math.pi, scalar2=-TWO_PI,
+            op0=ALU.is_gt, op1=ALU.mult,
+        )
+        nc.vector.tensor_add(out=phase[:], in0=phase[:], in1=wrap[:])
+        sin_cos = const.tile([P, 2, TOK_TILES, HALF_ROPE], F32, name="sin_cos")
+        nc.scalar.activation(
+            out=sin_cos[:].rearrange("p s i j -> p s (i j)"), in_=phase[:], func=ACT.Sin
+        )
+        nc.scalar.activation(out=table_warmer[:], in_=table_warmer[:], func=ACT.Sqrt)
+
+        ks_stage = [
+            [
+                keep.tile(
+                    [P, GROUP, HALF_TILES, NOPE + ROPE], F32, name="ks_stage%d%d" % (half, b)
+                )
+                for b in range(2)
+            ]
+            for half in range(HALVES)
+        ]
+        both = [P, TOK_TILES, 2, HALF_ROPE]
+        by_sin = const.tile(both, F32, name="by_sin")
+        by_cos = const.tile(both, F32, name="by_cos")
+        rotated = const.tile(both, F32, name="rotated")
+
+        def rotate_k_pe():
+            nc.vector.tensor_tensor(
+                out=by_sin[:], in0=kp[:], in1=sin_cos[:, 0].unsqueeze(2).to_broadcast(both),
+                op=ALU.mult,
+            )
+            nc.vector.tensor_tensor(
+                out=by_cos[:], in0=kp[:], in1=sin_cos[:, 1].unsqueeze(2).to_broadcast(both),
+                op=ALU.mult,
+            )
+            nc.vector.tensor_tensor(
+                out=rotated[:, :, 0, :], in0=by_cos[:, :, 0, :], in1=by_sin[:, :, 1, :],
+                op=ALU.subtract,
+            )
+            nc.vector.tensor_tensor(
+                out=rotated[:, :, 1, :], in0=by_sin[:, :, 0, :], in1=by_cos[:, :, 1, :],
+                op=ALU.add,
+            )
+
+        def fill_rope(half):
+            toks = slice(HALF_TILES * half, HALF_TILES * (half + 1))
+            for stage in ks_stage[half]:
+                nc.vector.tensor_copy(
+                    out=stage[:, :, :, NOPE:],
+                    in_=rotated[:, toks, :, :]
+                    .rearrange("p i s j -> p i (s j)")
+                    .unsqueeze(1)
+                    .to_broadcast([P, GROUP, HALF_TILES, ROPE]),
+                )
+
+        gain = const.tile([P, PACK, P], F32, name="gain")
+
+        def spread_gain():
+            gain_ps = psum.tile([P, KVR], F32, tag="bank", name="gain_ps")
+            nc.tensor.matmul(gain_ps[:], lhsT=ones[:], rhs=gain_row[:], start=True, stop=True)
+            nc.vector.tensor_copy(
+                out=gain[:], in_=gain_ps[:].rearrange("p (q t) -> p t q", t=PACK)
+            )
+
+        def codes_and_scales(name, width):
+            codes = keep.tile([P, width], U32, name=name + "_codes", align_bytes=64)
+            scales = keep.tile([P, width], U8, name=name + "_scales", align_bytes=64)
+            return codes, scales
+
+        x_q = [codes_and_scales("x%d" % i, X_PASSES * P) for i in range(TOK_TILES)]
+        wc_q = [codes_and_scales("wc%d" % g, KVR) for g in range(X_PASSES)]
+        cn_q = [codes_and_scales("cn%d" % i, P) for i in range(TOK_TILES)]
+        wv_q = [codes_and_scales("wv%d" % m, GROUP * VD) for m in range(GROUPS)]
+        wk_q = [codes_and_scales("wk%d" % m, GROUP * NOPE) for m in range(GROUPS)]
+
+        def quantise(grouped, pair):
+            codes, scales = pair
+            nc.vector.quantize_mx(
+                out=codes[:].bitcast(FP8X4), scales=scales[:], in_=grouped
+            )
+
+        def mx(out, lhs, lhs_cols, rhs, start, stop):
+            nc.tensor.matmul_mx(
+                out=out,
+                lhsT=lhs[0][:, lhs_cols].bitcast(FP8X4),
+                lhsT_scale=lhs[1][:, lhs_cols],
+                rhs=rhs[0][:].bitcast(FP8X4),
+                rhs_scale=rhs[1][:],
+                start=start,
+                stop=stop,
+            )
+
+        def leave_psum(which, out, in_):
+            if which % 2 == 0:
+                nc.scalar.copy(out=out, in_=in_)
+            else:
+                nc.vector.tensor_copy(out=out, in_=in_)
+
+        x_grouped = {}
+        cn_rows = {}
+
+        def transpose_x(i):
+            words = x_pairs[i // 2][:, i % 2, :].bitcast(F32)
+            grouped = work.tile(
+                [P, X_PASSES * P * PACK], BF16, tag="grouped", bufs=4, align_bytes=64,
+                name="x_grouped",
+            )
+            grouped_words = grouped[:].bitcast(F32)
+            for bank in range(2):
+                xt = psum.tile([P, 4, P], F32, tag="bank", name="xt")
+                for s in range(4):
+                    first = 2 * P * (2 * bank + s // 2)
+                    nc.tensor.transpose(
+                        xt[:, s, :], words[:, first + s % 2 : first + 2 * P : 2], ident_f32[:]
+                    )
+                leave_psum(
+                    0,
+                    grouped_words[:, 512 * bank : 512 * (bank + 1)].rearrange(
+                        "p (g r u) -> p g r u", g=2, u=2
+                    ),
+                    xt[:].rearrange("p (g u) r -> p g r u", u=2),
+                )
+            x_grouped[i] = grouped
+
+        def quantise_x(i):
+            quantise(x_grouped[i][:], x_q[i])
+
+        def project(i):
+            acc = psum.tile([P, KVR], F32, tag="bank", name="acc")
+            for g in range(X_PASSES):
+                mx(acc[:], x_q[i], slice(P * g, P * (g + 1)), wc_q[g],
+                   g == 0, g == X_PASSES - 1)
+            squares = work.tile([P, KVR], BF16, tag="squares", name="squares")
+            mean_sq = work.tile([P, 1], F32, tag="mean_sq", name="mean_sq")
+            nc.scalar.activation(
+                out=squares[:], in_=acc[:], func=ACT.Square,
+                scale=1.0 / math.sqrt(KVR), accum_out=mean_sq[:],
+            )
+            rms = work.tile([P, 1], F32, tag="rms", name="rms")
+            nc.scalar.activation(out=rms[:], in_=mean_sq[:], func=ACT.Sqrt, bias=EPS)
+            inv_rms = work.tile([P, 1], F32, tag="inv_rms", name="inv_rms")
+            nc.vector.reciprocal(out=inv_rms[:], in_=rms[:])
+            cn = work.tile([P, PACK, P], BF16, tag="cn", bufs=4, name="cn")
+            nc.vector.scalar_tensor_tensor(
+                out=cn[:],
+                in0=acc[:].rearrange("p (q t) -> p t q", t=PACK),
+                scalar=inv_rms[:, 0:1],
+                in1=gain[:],
+                op0=ALU.mult,
+                op1=ALU.mult,
+            )
+            cn_rows[i] = cn
+
+        def transpose_cn(i):
+            cn_t = psum.tile([P, PACK, P], BF16, tag="bank", name="cn_t")
+            for t in range(PACK):
+                nc.tensor.transpose(cn_t[:, t, :], cn_rows[i][:, t, :], ident_bf16[:])
+            grouped = work.tile(
+                [P, P, PACK], BF16, tag="cn_grouped", align_bytes=64, name="cn_grouped"
+            )
+            nc.scalar.copy(out=grouped[:], in_=cn_t[:].rearrange("p t r -> p r t"))
+            quantise(grouped[:].rearrange("p r t -> p (r t)"), cn_q[i])
+
+        def grouped_columns(width):
+            grouped = work.tile(
+                [P, X_PASSES * P * PACK], BF16, tag="grouped", bufs=4, align_bytes=64,
+                name="w_grouped",
+            )
+            return grouped[:, 0 : width * PACK]
+
+        def regroup_wc(g):
+            flat = grouped_columns(KVR)
+            dst = flat.rearrange("p (c i t) -> p c t i", i=RUN, t=PACK)
+            src = wc_raw[g][:].rearrange("p t (c i) -> p c t i", i=RUN)
+            middle = KVR // RUN // 2
+            nc.scalar.copy(out=dst[:, 0:middle], in_=src[:, 0:middle])
+            nc.vector.tensor_copy(out=dst[:, middle:], in_=src[:, middle:])
+            return flat
+
+        def regroup_wb(m, first, width):
+            flat = grouped_columns(GROUP * width)
+            heads = wb_raw[m][:].rearrange("p t (h f) -> p t h f", f=HEAD_COLS)
+            nc.vector.tensor_copy(
+                out=flat.rearrange("p (h c i t) -> p h c t i", h=GROUP, i=RUN, t=PACK),
+                in_=heads[:, :, :, first : first + width].rearrange(
+                    "p t h (c i) -> p h c t i", i=RUN
+                ),
+            )
+            return flat
+
+        def vector_takes(half, n):
+            if half == 0:
+                return 1 if n % 4 == 3 else 0
+            return n % 2
+
+        def v_unit(m, half):
+            stage = work.tile([P, GROUP, HALF_TILES, VD], F32, tag="v_stage", bufs=4,
+                              name="v_stage")
+            for s in range(HALF_TILES):
+                i = HALF_TILES * half + s
+                kv = psum.tile([P, GROUP * VD], F32, tag="bank", name="kv")
+                mx(kv[:], cn_q[i], slice(0, P), wv_q[m], True, True)
+                leave_psum(
+                    vector_takes(half, s),
+                    stage[:, :, s, :],
+                    kv[:].rearrange("p (h d) -> p h d", h=GROUP),
+                )
+            nc.sync.dma_start(
+                out=v_view[:, GROUP * m : GROUP * (m + 1),
+                           HALF_TILES * half : HALF_TILES * (half + 1), :],
+                in_=stage[:],
+            )
+
+        def k_unit(m, half):
+            stage = ks_stage[half][m % 2]
+            for pair in range(HALF_TILES // 2):
+                kk = psum.tile([P, 2, GROUP * NOPE], F32, tag="bank", name="kk")
+                for s in range(2):
+                    i = HALF_TILES * half + 2 * pair + s
+                    mx(kk[:, s, :], cn_q[i], slice(0, P), wk_q[m], True, True)
+                leave_psum(
+                    vector_takes(half, 2 + pair),
+                    stage[:, :, 2 * pair : 2 * pair + 2, 0:NOPE].rearrange("p h i d -> p i h d"),
+                    kk[:].rearrange("p i (h d) -> p i h d", h=GROUP),
+                )
+            nc.sync.dma_start(
+                out=ks_view[:, GROUP * m : GROUP * (m + 1),
+                            HALF_TILES * half : HALF_TILES * (half + 1), :],
+                in_=stage[:],
+            )
+
+        def unit(u, half):
+            if u % 2 == 0:
+                v_unit(u // 2, half)
+            else:
+                k_unit(u // 2, half)
+
+        unit_flats = {}
+
+        def regroup_unit(u):
+            if u % 2 == 0:
+                unit_flats[u] = regroup_wb(u // 2, NOPE, VD)
+            else:
+                unit_flats[u] = regroup_wb(u // 2, 0, NOPE)
+
+        def quantise_unit(u):
+            quantise(unit_flats[u], wv_q[u // 2] if u % 2 == 0 else wk_q[u // 2])
+
+        units = 2 * GROUPS
+        second = HALF_TILES
+
+        spread_gain()
+        flats = {}
+        for g in range(X_PASSES):
+            flats[g] = regroup_wc(g)
+            if g > 0:
+                quantise(flats[g - 1], wc_q[g - 1])
+        quantise(flats[X_PASSES - 1], wc_q[X_PASSES - 1])
+        rotate_k_pe()
+
+        for i in range(HALF_TILES):
+            transpose_x(i)
+        quantise_x(0)
+        fill_rope(0)
+        quantise_x(1)
+        quantise_x(2)
+        regroup_unit(0)
+        quantise_x(3)
+        quantise_unit(0)
+        for i in range(HALF_TILES):
+            project(i)
+        for i in range(HALF_TILES):
+            transpose_cn(i)
+        regroup_unit(1)
+
+        for u in range(units):
+            if u + 1 < units:
+                quantise_unit(u + 1)
+            unit(u, 0)
+            if u + 2 < units:
+                regroup_unit(u + 2)
+            if u < HALF_TILES:
+                transpose_x(second + u)
+            if 1 <= u < HALF_TILES + 1:
+                quantise_x(second + u - 1)
+            if 2 <= u < HALF_TILES + 2:
+                project(second + u - 2)
+            if u >= HALF_TILES:
+                transpose_cn(u)
+
+        fill_rope(1)
+        for u in range(units):
+            unit(u, 1)

@@ -28,12 +28,12 @@ X_PASSES = D // K_PASS
 HEAD_COLS = NOPE + VD
 GROUP = 4
 GROUPS = H // GROUP
+PAIR = 2
 HALVES = 2
 HALF_TILES = TOK_TILES // HALVES
+HALF_GROUPS = 4
 
 TWO_PI = 2.0 * math.pi
-TWO_PI_HI = 6.28125
-TWO_PI_LO = TWO_PI - TWO_PI_HI
 
 FLOPS = 2 * T * D * KVR + 2 * T * KVR * H * HEAD_COLS
 
@@ -54,34 +54,41 @@ def tile_deepseekmultiheadattention_pb_kernel(
         ks_view = out_0.rearrange("b h (p i) d -> p (b h) i d", i=TOK_TILES)
         v_view = out_1.rearrange("b h (p i) d -> p (b h) i d", i=TOK_TILES)
 
-        gain_row = const.tile([P, KVR], BF16, name="gain_row")
-        nc.vector.memset(gain_row[:], 0.0)
-        nc.sync.dma_start(
-            out=gain_row[0:1, :], in_=kv_a_norm_w.rearrange("(o n) -> o n", o=1)
-        )
         kp = const.tile([P, TOK_TILES, 2, HALF_ROPE], BF16, name="kp")
-        nc.sync.dma_start(
+        nc.scalar.dma_start(
             out=kp[:],
             in_=k_pe.rearrange("b (p i) (s j) -> p (b i) s j", i=TOK_TILES, s=2),
         )
+        gain_row = const.tile([P, KVR], BF16, name="gain_row")
+        nc.gpsimd.memset(gain_row[:], 0.0)
+        nc.scalar.dma_start(
+            out=gain_row[0:1, :], in_=kv_a_norm_w.rearrange("(o n) -> o n", o=1)
+        )
 
-        x_pairs = [
-            keep.tile([P, 2, D], BF16, name="x_pair%d" % j) for j in range(TOK_TILES // 2)
-        ]
+        x_single = [keep.tile([P, D], BF16, name="x_single%d" % i) for i in range(HALF_TILES)]
+        x_pairs = [keep.tile([P, 2, D], BF16, name="x_pair%d" % j) for j in range(2)]
         wc_raw = [
             keep.tile([P, PACK, KVR], BF16, name="wc_raw%d" % g) for g in range(X_PASSES)
         ]
+        wb_groups = [(0, 1), (1, 1), (2, 2)]
         wb_raw = [
-            keep.tile([P, PACK, GROUP * HEAD_COLS], BF16, name="wb_raw%d" % m)
-            for m in range(GROUPS)
+            keep.tile([P, PACK, n * GROUP * HEAD_COLS], BF16, name="wb_raw%d" % first)
+            for first, n in wb_groups
         ]
 
-        def load_x_pair(j):
-            nc.sync.dma_start(out=x_pairs[j][:], in_=x_view[:, 2 * j : 2 * j + 2, :])
+        def load_wb(w):
+            first, n = wb_groups[w]
+            cols = slice(GROUP * HEAD_COLS * first, GROUP * HEAD_COLS * (first + n))
+            nc.sync.dma_start(out=wb_raw[w][:], in_=wb_view[:, :, cols])
 
-        def load_wb(m):
-            cols = slice(GROUP * HEAD_COLS * m, GROUP * HEAD_COLS * (m + 1))
-            nc.sync.dma_start(out=wb_raw[m][:], in_=wb_view[:, :, cols])
+        def load_x_pair(j):
+            first = HALF_TILES + 2 * j
+            nc.sync.dma_start(out=x_pairs[j][:], in_=x_view[:, first : first + 2, :])
+
+        def x_rows(i):
+            if i < HALF_TILES:
+                return x_single[i][:]
+            return x_pairs[(i - HALF_TILES) // 2][:, i % 2, :]
 
         for g in range(X_PASSES):
             nc.sync.dma_start(
@@ -90,18 +97,21 @@ def tile_deepseekmultiheadattention_pb_kernel(
                     "(q t) c -> q t c", t=PACK
                 ),
             )
+        for i in range(HALF_TILES):
+            nc.sync.dma_start(out=x_single[i][:], in_=x_view[:, i, :])
+        load_wb(0)
         load_x_pair(0)
         load_x_pair(1)
-        load_wb(0)
-        load_x_pair(2)
-        load_x_pair(3)
-        for m in range(1, GROUPS):
-            load_wb(m)
+        load_wb(1)
+        load_wb(2)
 
+        minus_half = const.tile([P, 1], F32, name="minus_half")
+        nc.vector.memset(minus_half[:], -0.5)
         ones = const.tile([P, P], BF16, name="ones")
         nc.vector.memset(ones[:], 1.0)
         table_warmer = const.tile([P, 1], F32, name="table_warmer")
-        nc.vector.memset(table_warmer[:], 1.0)
+        nc.vector.memset(table_warmer[:], 0.0)
+        nc.scalar.activation(out=table_warmer[:], in_=table_warmer[:], func=ACT.Sin)
 
         pos = const.tile([P, TOK_TILES], F32, name="pos")
         nc.gpsimd.iota(
@@ -115,61 +125,34 @@ def tile_deepseekmultiheadattention_pb_kernel(
         make_identity(nc, ident_f32[:])
         ident_bf16 = const.tile([P, P], BF16, name="ident_bf16")
         make_identity(nc, ident_bf16[:])
-        angle = const.tile([P, TOK_TILES, HALF_ROPE], F32, name="angle")
-        nc.vector.tensor_copy(out=angle[:, :, 0], in_=pos[:])
+        angles = [P, 2, TOK_TILES, HALF_ROPE]
+        turns = const.tile(angles, F32, name="turns")
+        nc.vector.tensor_scalar_mul(out=turns[:, 0, :, 0], in0=pos[:], scalar1=1.0 / TWO_PI)
         for step in range(5):
             width = 2 ** step
             nc.vector.tensor_scalar_mul(
-                out=angle[:, :, width : 2 * width],
-                in0=angle[:, :, 0:width],
+                out=turns[:, 0, :, width : 2 * width],
+                in0=turns[:, 0, :, 0:width],
                 scalar1=ROPE_BASE ** (-width / HALF_ROPE),
             )
-        angle_flat = angle[:].rearrange("p i j -> p (i j)")
-        n_angles = TOK_TILES * HALF_ROPE
-        turns = const.tile([P, n_angles], I32, name="turns")
-        nc.vector.tensor_scalar(
-            out=turns[:], in0=angle_flat, scalar1=1.0 / TWO_PI, scalar2=None, op0=ALU.mult
-        )
-        coarse = const.tile([P, n_angles], F32, name="coarse")
-        nc.vector.scalar_tensor_tensor(
-            out=coarse[:], in0=turns[:], scalar=-TWO_PI_HI, in1=angle_flat,
-            op0=ALU.mult, op1=ALU.add,
-        )
-        phase = const.tile([P, 2, n_angles], F32, name="phase")
-        nc.vector.scalar_tensor_tensor(
-            out=phase[:, 0, :], in0=turns[:], scalar=-TWO_PI_LO, in1=coarse[:],
-            op0=ALU.mult, op1=ALU.add,
-        )
-        nc.vector.tensor_scalar_add(
-            out=phase[:, 1, :], in0=phase[:, 0, :], scalar1=math.pi / 2.0
-        )
-        wrap = const.tile([P, 2, n_angles], F32, name="wrap")
-        nc.vector.tensor_scalar(
-            out=wrap[:], in0=phase[:], scalar1=math.pi, scalar2=-TWO_PI,
-            op0=ALU.is_gt, op1=ALU.mult,
-        )
-        nc.vector.tensor_add(out=phase[:], in0=phase[:], in1=wrap[:])
-        sin_cos = const.tile([P, 2, TOK_TILES, HALF_ROPE], F32, name="sin_cos")
-        nc.scalar.activation(
-            out=sin_cos[:].rearrange("p s i j -> p s (i j)"), in_=phase[:], func=ACT.Sin
-        )
-        nc.scalar.activation(out=table_warmer[:], in_=table_warmer[:], func=ACT.Sqrt)
+        nc.vector.tensor_scalar_add(out=turns[:, 1], in0=turns[:, 0], scalar1=0.25)
+        whole = const.tile(angles, I32, name="whole")
+        nc.vector.tensor_copy(out=whole[:], in_=turns[:])
+        phase = const.tile(angles, F32, name="phase")
+        nc.vector.tensor_tensor(out=phase[:], in0=turns[:], in1=whole[:], op=ALU.subtract)
+        sin_cos = const.tile(angles, F32, name="sin_cos")
+        nc.scalar.activation(out=sin_cos[:], in_=phase[:], func=ACT.Sin, scale=TWO_PI)
 
         ks_stage = [
-            [
-                keep.tile(
-                    [P, GROUP, HALF_TILES, NOPE + ROPE], F32, name="ks_stage%d%d" % (half, b)
-                )
-                for b in range(2)
-            ]
-            for half in range(HALVES)
+            keep.tile([P, GROUP, TOK_TILES, NOPE + ROPE], F32, name="ks_stage%d" % b)
+            for b in range(2)
         ]
         both = [P, TOK_TILES, 2, HALF_ROPE]
         by_sin = const.tile(both, F32, name="by_sin")
         by_cos = const.tile(both, F32, name="by_cos")
         rotated = const.tile(both, F32, name="rotated")
 
-        def rotate_k_pe():
+        def multiply_k_pe():
             nc.vector.tensor_tensor(
                 out=by_sin[:], in0=kp[:], in1=sin_cos[:, 0].unsqueeze(2).to_broadcast(both),
                 op=ALU.mult,
@@ -178,6 +161,8 @@ def tile_deepseekmultiheadattention_pb_kernel(
                 out=by_cos[:], in0=kp[:], in1=sin_cos[:, 1].unsqueeze(2).to_broadcast(both),
                 op=ALU.mult,
             )
+
+        def rotate_k_pe():
             nc.vector.tensor_tensor(
                 out=rotated[:, :, 0, :], in0=by_cos[:, :, 0, :], in1=by_sin[:, :, 1, :],
                 op=ALU.subtract,
@@ -187,25 +172,22 @@ def tile_deepseekmultiheadattention_pb_kernel(
                 op=ALU.add,
             )
 
-        def fill_rope(half):
+        def fill_rope(b, half):
             toks = slice(HALF_TILES * half, HALF_TILES * (half + 1))
-            for stage in ks_stage[half]:
-                nc.vector.tensor_copy(
-                    out=stage[:, :, :, NOPE:],
-                    in_=rotated[:, toks, :, :]
-                    .rearrange("p i s j -> p i (s j)")
-                    .unsqueeze(1)
-                    .to_broadcast([P, GROUP, HALF_TILES, ROPE]),
-                )
+            nc.vector.tensor_copy(
+                out=ks_stage[b][:, :, toks, NOPE:],
+                in_=rotated[:, toks, :, :]
+                .rearrange("p i s j -> p i (s j)")
+                .unsqueeze(1)
+                .to_broadcast([P, GROUP, HALF_TILES, ROPE]),
+            )
 
         gain = const.tile([P, PACK, P], F32, name="gain")
 
         def spread_gain():
             gain_ps = psum.tile([P, KVR], F32, tag="bank", name="gain_ps")
             nc.tensor.matmul(gain_ps[:], lhsT=ones[:], rhs=gain_row[:], start=True, stop=True)
-            nc.vector.tensor_copy(
-                out=gain[:], in_=gain_ps[:].rearrange("p (q t) -> p t q", t=PACK)
-            )
+            nc.scalar.copy(out=gain[:], in_=gain_ps[:].rearrange("p (q t) -> p t q", t=PACK))
 
         def codes_and_scales(name, width):
             codes = keep.tile([P, width], U32, name=name + "_codes", align_bytes=64)
@@ -224,30 +206,31 @@ def tile_deepseekmultiheadattention_pb_kernel(
                 out=codes[:].bitcast(FP8X4), scales=scales[:], in_=grouped
             )
 
-        def mx(out, lhs, lhs_cols, rhs, start, stop):
+        def mx(out, lhs, lhs_cols, rhs, rhs_cols, start, stop):
             nc.tensor.matmul_mx(
                 out=out,
                 lhsT=lhs[0][:, lhs_cols].bitcast(FP8X4),
                 lhsT_scale=lhs[1][:, lhs_cols],
-                rhs=rhs[0][:].bitcast(FP8X4),
-                rhs_scale=rhs[1][:],
+                rhs=rhs[0][:, rhs_cols].bitcast(FP8X4),
+                rhs_scale=rhs[1][:, rhs_cols],
                 start=start,
                 stop=stop,
             )
 
-        def leave_psum(which, out, in_):
-            if which % 2 == 0:
+        def leave_psum(n, share, out, in_):
+            if n % share < share - 1:
                 nc.scalar.copy(out=out, in_=in_)
             else:
                 nc.vector.tensor_copy(out=out, in_=in_)
 
         x_grouped = {}
         cn_rows = {}
+        cn_grouped = {}
 
         def transpose_x(i):
-            words = x_pairs[i // 2][:, i % 2, :].bitcast(F32)
+            words = x_rows(i).bitcast(F32)
             grouped = work.tile(
-                [P, X_PASSES * P * PACK], BF16, tag="grouped", bufs=4, align_bytes=64,
+                [P, X_PASSES * P * PACK], BF16, tag="grouped", bufs=5, align_bytes=64,
                 name="x_grouped",
             )
             grouped_words = grouped[:].bitcast(F32)
@@ -258,38 +241,47 @@ def tile_deepseekmultiheadattention_pb_kernel(
                     nc.tensor.transpose(
                         xt[:, s, :], words[:, first + s % 2 : first + 2 * P : 2], ident_f32[:]
                     )
-                leave_psum(
-                    0,
-                    grouped_words[:, 512 * bank : 512 * (bank + 1)].rearrange(
+                nc.scalar.copy(
+                    out=grouped_words[:, 512 * bank : 512 * (bank + 1)].rearrange(
                         "p (g r u) -> p g r u", g=2, u=2
                     ),
-                    xt[:].rearrange("p (g u) r -> p g r u", u=2),
+                    in_=xt[:].rearrange("p (g u) r -> p g r u", u=2),
                 )
             x_grouped[i] = grouped
 
         def quantise_x(i):
             quantise(x_grouped[i][:], x_q[i])
 
+        acc_of = {}
+        inv_rms_of = {}
+
         def project(i):
             acc = psum.tile([P, KVR], F32, tag="bank", name="acc")
             for g in range(X_PASSES):
-                mx(acc[:], x_q[i], slice(P * g, P * (g + 1)), wc_q[g],
+                mx(acc[:], x_q[i], slice(P * g, P * (g + 1)), wc_q[g], slice(0, KVR),
                    g == 0, g == X_PASSES - 1)
             squares = work.tile([P, KVR], BF16, tag="squares", name="squares")
-            mean_sq = work.tile([P, 1], F32, tag="mean_sq", name="mean_sq")
+            mean_sq = work.tile([P, 1], F32, tag="mean_sq", bufs=4, name="mean_sq")
             nc.scalar.activation(
                 out=squares[:], in_=acc[:], func=ACT.Square,
                 scale=1.0 / math.sqrt(KVR), accum_out=mean_sq[:],
             )
-            rms = work.tile([P, 1], F32, tag="rms", name="rms")
-            nc.scalar.activation(out=rms[:], in_=mean_sq[:], func=ACT.Sqrt, bias=EPS)
-            inv_rms = work.tile([P, 1], F32, tag="inv_rms", name="inv_rms")
-            nc.vector.reciprocal(out=inv_rms[:], in_=rms[:])
+            shifted = work.tile([P, 1], F32, tag="shifted", bufs=4, name="shifted")
+            nc.gpsimd.tensor_scalar_add(out=shifted[:], in0=mean_sq[:], scalar1=EPS)
+            inv_rms = work.tile([P, 1], F32, tag="inv_rms", bufs=4, name="inv_rms")
+            nc.gpsimd.tensor_tensor(
+                out=inv_rms[:], in0=shifted[:], in1=minus_half[:], op=ALU.pow
+            )
+            acc_of[i] = acc
+            inv_rms_of[i] = inv_rms
+
+        def normalise(i):
+            acc = acc_of[i]
             cn = work.tile([P, PACK, P], BF16, tag="cn", bufs=4, name="cn")
             nc.vector.scalar_tensor_tensor(
                 out=cn[:],
                 in0=acc[:].rearrange("p (q t) -> p t q", t=PACK),
-                scalar=inv_rms[:, 0:1],
+                scalar=inv_rms_of[i][:, 0:1],
                 in1=gain[:],
                 op0=ALU.mult,
                 op1=ALU.mult,
@@ -301,14 +293,17 @@ def tile_deepseekmultiheadattention_pb_kernel(
             for t in range(PACK):
                 nc.tensor.transpose(cn_t[:, t, :], cn_rows[i][:, t, :], ident_bf16[:])
             grouped = work.tile(
-                [P, P, PACK], BF16, tag="cn_grouped", align_bytes=64, name="cn_grouped"
+                [P, P, PACK], BF16, tag="cn_grouped", bufs=4, align_bytes=64, name="cn_grouped"
             )
             nc.scalar.copy(out=grouped[:], in_=cn_t[:].rearrange("p t r -> p r t"))
-            quantise(grouped[:].rearrange("p r t -> p (r t)"), cn_q[i])
+            cn_grouped[i] = grouped
+
+        def quantise_cn(i):
+            quantise(cn_grouped[i][:].rearrange("p r t -> p (r t)"), cn_q[i])
 
         def grouped_columns(width):
             grouped = work.tile(
-                [P, X_PASSES * P * PACK], BF16, tag="grouped", bufs=4, align_bytes=64,
+                [P, X_PASSES * P * PACK], BF16, tag="grouped", bufs=5, align_bytes=64,
                 name="w_grouped",
             )
             return grouped[:, 0 : width * PACK]
@@ -324,31 +319,26 @@ def tile_deepseekmultiheadattention_pb_kernel(
 
         def regroup_wb(m, first, width):
             flat = grouped_columns(GROUP * width)
-            heads = wb_raw[m][:].rearrange("p t (h f) -> p t h f", f=HEAD_COLS)
+            w = min(m, 2)
+            head = GROUP * (m - wb_groups[w][0])
+            heads = wb_raw[w][:].rearrange("p t (h f) -> p t h f", f=HEAD_COLS)
             nc.vector.tensor_copy(
                 out=flat.rearrange("p (h c i t) -> p h c t i", h=GROUP, i=RUN, t=PACK),
-                in_=heads[:, :, :, first : first + width].rearrange(
+                in_=heads[:, :, head : head + GROUP, first : first + width].rearrange(
                     "p t h (c i) -> p h c t i", i=RUN
                 ),
             )
             return flat
 
-        def vector_takes(half, n):
-            if half == 0:
-                return 1 if n % 4 == 3 else 0
-            return n % 2
-
-        def v_unit(m, half):
+        def v_half(m, half, share):
             stage = work.tile([P, GROUP, HALF_TILES, VD], F32, tag="v_stage", bufs=4,
                               name="v_stage")
             for s in range(HALF_TILES):
                 i = HALF_TILES * half + s
                 kv = psum.tile([P, GROUP * VD], F32, tag="bank", name="kv")
-                mx(kv[:], cn_q[i], slice(0, P), wv_q[m], True, True)
+                mx(kv[:], cn_q[i], slice(0, P), wv_q[m], slice(0, GROUP * VD), True, True)
                 leave_psum(
-                    vector_takes(half, s),
-                    stage[:, :, s, :],
-                    kv[:].rearrange("p (h d) -> p h d", h=GROUP),
+                    s, share, stage[:, :, s, :], kv[:].rearrange("p (h d) -> p h d", h=GROUP)
                 )
             nc.sync.dma_start(
                 out=v_view[:, GROUP * m : GROUP * (m + 1),
@@ -356,83 +346,121 @@ def tile_deepseekmultiheadattention_pb_kernel(
                 in_=stage[:],
             )
 
-        def k_unit(m, half):
-            stage = ks_stage[half][m % 2]
-            for pair in range(HALF_TILES // 2):
-                kk = psum.tile([P, 2, GROUP * NOPE], F32, tag="bank", name="kk")
+        def v_pair(m, pair):
+            stage = work.tile([P, PAIR, TOK_TILES, VD], F32, tag="v_stage", bufs=4,
+                              name="v_stage")
+            width = PAIR * VD
+            for b in range(TOK_TILES // 2):
+                kv = psum.tile([P, 2, width], F32, tag="bank", name="kv")
                 for s in range(2):
-                    i = HALF_TILES * half + 2 * pair + s
-                    mx(kk[:, s, :], cn_q[i], slice(0, P), wk_q[m], True, True)
+                    mx(kv[:, s, :], cn_q[2 * b + s], slice(0, P), wv_q[m],
+                       slice(width * pair, width * (pair + 1)), True, True)
                 leave_psum(
-                    vector_takes(half, 2 + pair),
-                    stage[:, :, 2 * pair : 2 * pair + 2, 0:NOPE].rearrange("p h i d -> p i h d"),
+                    b, 2,
+                    stage[:, :, 2 * b : 2 * b + 2, :].rearrange("p h i d -> p i h d"),
+                    kv[:].rearrange("p i (h d) -> p i h d", h=PAIR),
+                )
+            head = GROUP * m + PAIR * pair
+            nc.sync.dma_start(out=v_view[:, head : head + PAIR, :, :], in_=stage[:])
+
+        def k_tiles(m, first, tiles, share):
+            stage = ks_stage[m % 2]
+            for b in range(tiles // 2):
+                kk = psum.tile([P, 2, GROUP * NOPE], F32, tag="bank", name="kk")
+                at = first + 2 * b
+                for s in range(2):
+                    mx(kk[:, s, :], cn_q[at + s], slice(0, P), wk_q[m],
+                       slice(0, GROUP * NOPE), True, True)
+                leave_psum(
+                    b, share,
+                    stage[:, :, at : at + 2, 0:NOPE].rearrange("p h i d -> p i h d"),
                     kk[:].rearrange("p i (h d) -> p i h d", h=GROUP),
                 )
             nc.sync.dma_start(
-                out=ks_view[:, GROUP * m : GROUP * (m + 1),
-                            HALF_TILES * half : HALF_TILES * (half + 1), :],
-                in_=stage[:],
+                out=ks_view[:, GROUP * m : GROUP * (m + 1), first : first + tiles, :],
+                in_=stage[:, :, first : first + tiles, :],
             )
 
-        def unit(u, half):
-            if u % 2 == 0:
-                v_unit(u // 2, half)
-            else:
-                k_unit(u // 2, half)
+        flat_of = {}
 
-        unit_flats = {}
+        def regroup_v(m):
+            flat_of[m, 0] = regroup_wb(m, NOPE, VD)
+
+        def regroup_k(m):
+            flat_of[m, 1] = regroup_wb(m, 0, NOPE)
+
+        def quantise_v(m):
+            quantise(flat_of[m, 0], wv_q[m])
+
+        def quantise_k(m):
+            quantise(flat_of[m, 1], wk_q[m])
+
+        def unit(u, half, share):
+            if u % 2 == 0:
+                v_half(u // 2, half, share)
+            else:
+                k_tiles(u // 2, HALF_TILES * half, HALF_TILES, share)
 
         def regroup_unit(u):
             if u % 2 == 0:
-                unit_flats[u] = regroup_wb(u // 2, NOPE, VD)
+                regroup_v(u // 2)
             else:
-                unit_flats[u] = regroup_wb(u // 2, 0, NOPE)
+                regroup_k(u // 2)
 
         def quantise_unit(u):
-            quantise(unit_flats[u], wv_q[u // 2] if u % 2 == 0 else wk_q[u // 2])
+            if u % 2 == 0:
+                quantise_v(u // 2)
+            else:
+                quantise_k(u // 2)
 
-        units = 2 * GROUPS
-        second = HALF_TILES
-
-        spread_gain()
         flats = {}
         for g in range(X_PASSES):
             flats[g] = regroup_wc(g)
             if g > 0:
                 quantise(flats[g - 1], wc_q[g - 1])
         quantise(flats[X_PASSES - 1], wc_q[X_PASSES - 1])
-        rotate_k_pe()
-
+        multiply_k_pe()
         for i in range(HALF_TILES):
             transpose_x(i)
         quantise_x(0)
-        fill_rope(0)
+        rotate_k_pe()
         quantise_x(1)
         quantise_x(2)
-        regroup_unit(0)
+        regroup_v(0)
         quantise_x(3)
-        quantise_unit(0)
+        spread_gain()
         for i in range(HALF_TILES):
             project(i)
+        normalise(0)
+        quantise_v(0)
+        normalise(1)
+        normalise(2)
+        regroup_k(0)
+        normalise(3)
         for i in range(HALF_TILES):
             transpose_cn(i)
-        regroup_unit(1)
-
-        for u in range(units):
-            if u + 1 < units:
+        for i in range(HALF_TILES):
+            quantise_cn(i)
+        for u in range(8):
+            if u + 1 < 8:
                 quantise_unit(u + 1)
-            unit(u, 0)
-            if u + 2 < units:
+            if u < 2:
+                fill_rope(u, 0)
+            unit(u, 0, 2 if u == 0 else 4)
+            if u + 2 < 8:
                 regroup_unit(u + 2)
-            if u < HALF_TILES:
-                transpose_x(second + u)
-            if 1 <= u < HALF_TILES + 1:
-                quantise_x(second + u - 1)
-            if 2 <= u < HALF_TILES + 2:
-                project(second + u - 2)
-            if u >= HALF_TILES:
+            if u < 4:
+                transpose_x(4 + u)
+            if 1 <= u < 5:
+                quantise_x(3 + u)
+            if 3 <= u < 7:
+                normalise(1 + u)
+            if 2 <= u < 6:
+                project(2 + u)
+            if 4 <= u:
                 transpose_cn(u)
-
-        fill_rope(1)
-        for u in range(units):
-            unit(u, 1)
+                quantise_cn(u)
+        fill_rope(0, 1)
+        fill_rope(1, 1)
+        for u in range(8):
+            unit(u, 1, 2)

@@ -59,11 +59,7 @@ def tile_deepseekmultiheadattention_pb_kernel(
             out=kp[:],
             in_=k_pe.rearrange("b (p i) (s j) -> p (b i) s j", i=TOK_TILES, s=2),
         )
-        gain_row = const.tile([P, KVR], BF16, name="gain_row")
-        nc.gpsimd.memset(gain_row[:], 0.0)
-        nc.scalar.dma_start(
-            out=gain_row[0:1, :], in_=kv_a_norm_w.rearrange("(o n) -> o n", o=1)
-        )
+
 
         x_single = [keep.tile([P, D], BF16, name="x_single%d" % i) for i in range(HALF_TILES)]
         x_pairs = [keep.tile([P, 2, D], BF16, name="x_pair%d" % j) for j in range(2)]
@@ -90,15 +86,25 @@ def tile_deepseekmultiheadattention_pb_kernel(
                 return x_single[i][:]
             return x_pairs[(i - HALF_TILES) // 2][:, i % 2, :]
 
-        for g in range(X_PASSES):
+        def load_wc(g):
             nc.sync.dma_start(
                 out=wc_raw[g][:],
                 in_=wkv_c[K_PASS * g : K_PASS * (g + 1), :].rearrange(
                     "(q t) c -> q t c", t=PACK
                 ),
             )
-        for i in range(HALF_TILES):
+
+        def load_x(i):
             nc.sync.dma_start(out=x_single[i][:], in_=x_view[:, i, :])
+
+        load_wc(0)
+        load_wc(1)
+        load_wc(2)
+        load_wc(3)
+        load_x(0)
+        load_x(1)
+        load_x(2)
+        load_x(3)
         load_wb(0)
         load_x_pair(0)
         load_x_pair(1)
@@ -120,6 +126,11 @@ def tile_deepseekmultiheadattention_pb_kernel(
             base=0,
             channel_multiplier=TOK_TILES,
             allow_small_or_imprecise_dtypes=True,
+        )
+        gain_row = const.tile([P, KVR], BF16, name="gain_row")
+        nc.gpsimd.memset(gain_row[:], 0.0)
+        nc.gpsimd.dma_start(
+            out=gain_row[0:1, :], in_=kv_a_norm_w.rearrange("(o n) -> o n", o=1)
         )
         ident_f32 = const.tile([P, P], F32, name="ident_f32")
         make_identity(nc, ident_f32[:])
@@ -227,14 +238,15 @@ def tile_deepseekmultiheadattention_pb_kernel(
         cn_rows = {}
         cn_grouped = {}
 
-        def transpose_x(i):
+        def transpose_x(i, banks=(0, 1)):
             words = x_rows(i).bitcast(F32)
-            grouped = work.tile(
-                [P, X_PASSES * P * PACK], BF16, tag="grouped", bufs=5, align_bytes=64,
-                name="x_grouped",
-            )
-            grouped_words = grouped[:].bitcast(F32)
-            for bank in range(2):
+            if banks[0] == 0:
+                x_grouped[i] = work.tile(
+                    [P, X_PASSES * P * PACK], BF16, tag="grouped", bufs=5, align_bytes=64,
+                    name="x_grouped",
+                )
+            grouped_words = x_grouped[i][:].bitcast(F32)
+            for bank in banks:
                 xt = psum.tile([P, 4, P], F32, tag="bank", name="xt")
                 for s in range(4):
                     first = 2 * P * (2 * bank + s // 2)
@@ -247,7 +259,6 @@ def tile_deepseekmultiheadattention_pb_kernel(
                     ),
                     in_=xt[:].rearrange("p (g u) r -> p g r u", u=2),
                 )
-            x_grouped[i] = grouped
 
         def quantise_x(i):
             quantise(x_grouped[i][:], x_q[i])
@@ -317,17 +328,19 @@ def tile_deepseekmultiheadattention_pb_kernel(
             nc.vector.tensor_copy(out=dst[:, middle:], in_=src[:, middle:])
             return flat
 
-        def regroup_wb(m, first, width):
+        def regroup_wb(m, first, width, on_scalar):
             flat = grouped_columns(GROUP * width)
             w = min(m, 2)
             head = GROUP * (m - wb_groups[w][0])
             heads = wb_raw[w][:].rearrange("p t (h f) -> p t h f", f=HEAD_COLS)
-            nc.vector.tensor_copy(
-                out=flat.rearrange("p (h c i t) -> p h c t i", h=GROUP, i=RUN, t=PACK),
-                in_=heads[:, :, head : head + GROUP, first : first + width].rearrange(
-                    "p t h (c i) -> p h c t i", i=RUN
-                ),
+            dst = flat.rearrange("p (h c i t) -> p h c t i", h=GROUP, i=RUN, t=PACK)
+            src = heads[:, :, head : head + GROUP, first : first + width].rearrange(
+                "p t h (c i) -> p h c t i", i=RUN
             )
+            if on_scalar:
+                nc.scalar.copy(out=dst, in_=src)
+            else:
+                nc.vector.tensor_copy(out=dst, in_=src)
             return flat
 
         def v_half(m, half, share):
@@ -383,11 +396,11 @@ def tile_deepseekmultiheadattention_pb_kernel(
 
         flat_of = {}
 
-        def regroup_v(m):
-            flat_of[m, 0] = regroup_wb(m, NOPE, VD)
+        def regroup_v(m, on_scalar=False):
+            flat_of[m, 0] = regroup_wb(m, NOPE, VD, on_scalar)
 
-        def regroup_k(m):
-            flat_of[m, 1] = regroup_wb(m, 0, NOPE)
+        def regroup_k(m, on_scalar=False):
+            flat_of[m, 1] = regroup_wb(m, 0, NOPE, on_scalar)
 
         def quantise_v(m):
             quantise(flat_of[m, 0], wv_q[m])
@@ -414,16 +427,19 @@ def tile_deepseekmultiheadattention_pb_kernel(
                 quantise_k(u // 2)
 
         flats = {}
+        multiply_k_pe()
         for g in range(X_PASSES):
             flats[g] = regroup_wc(g)
-            if g > 0:
+            if g == 0:
+                rotate_k_pe()
+            else:
                 quantise(flats[g - 1], wc_q[g - 1])
         quantise(flats[X_PASSES - 1], wc_q[X_PASSES - 1])
-        multiply_k_pe()
+        fill_rope(0, 0)
         for i in range(HALF_TILES):
             transpose_x(i)
         quantise_x(0)
-        rotate_k_pe()
+        fill_rope(1, 0)
         quantise_x(1)
         quantise_x(2)
         regroup_v(0)
@@ -431,11 +447,12 @@ def tile_deepseekmultiheadattention_pb_kernel(
         spread_gain()
         for i in range(HALF_TILES):
             project(i)
+            if i == 0:
+                regroup_k(0, True)
         normalise(0)
         quantise_v(0)
         normalise(1)
         normalise(2)
-        regroup_k(0)
         normalise(3)
         for i in range(HALF_TILES):
             transpose_cn(i)
@@ -444,22 +461,21 @@ def tile_deepseekmultiheadattention_pb_kernel(
         for u in range(8):
             if u + 1 < 8:
                 quantise_unit(u + 1)
-            if u < 2:
-                fill_rope(u, 0)
             unit(u, 0, 2 if u == 0 else 4)
+            if 3 <= u < 7:
+                normalise(u + 1)
             if u + 2 < 8:
                 regroup_unit(u + 2)
             if u < 4:
-                transpose_x(4 + u)
+                transpose_x(u + 4)
             if 1 <= u < 5:
-                quantise_x(3 + u)
-            if 3 <= u < 7:
-                normalise(1 + u)
+                quantise_x(u + 3)
             if 2 <= u < 6:
-                project(2 + u)
-            if 4 <= u:
-                transpose_cn(u)
-                quantise_cn(u)
+                project(u + 2)
+            if 4 <= u < 8:
+                transpose_cn(u + 0)
+            if 4 <= u < 8:
+                quantise_cn(u + 0)
         fill_rope(0, 1)
         fill_rope(1, 1)
         for u in range(8):

@@ -59,6 +59,11 @@ def tile_deepseekmultiheadattention_pb_kernel(
             out=kp[:],
             in_=k_pe.rearrange("b (p i) (s j) -> p (b i) s j", i=TOK_TILES, s=2),
         )
+        gain_row = const.tile([P, KVR], BF16, name="gain_row")
+        nc.gpsimd.memset(gain_row[:], 0.0)
+        nc.scalar.dma_start(
+            out=gain_row[0:1, :], in_=kv_a_norm_w.rearrange("(o n) -> o n", o=1)
+        )
 
 
         x_single = [keep.tile([P, D], BF16, name="x_single%d" % i) for i in range(HALF_TILES)]
@@ -126,11 +131,6 @@ def tile_deepseekmultiheadattention_pb_kernel(
             base=0,
             channel_multiplier=TOK_TILES,
             allow_small_or_imprecise_dtypes=True,
-        )
-        gain_row = const.tile([P, KVR], BF16, name="gain_row")
-        nc.gpsimd.memset(gain_row[:], 0.0)
-        nc.gpsimd.dma_start(
-            out=gain_row[0:1, :], in_=kv_a_norm_w.rearrange("(o n) -> o n", o=1)
         )
         ident_f32 = const.tile([P, P], F32, name="ident_f32")
         make_identity(nc, ident_f32[:])

@@ -60,7 +60,7 @@ def tile_deepseekmultiheadattention_pb_kernel(
             in_=k_pe.rearrange("b (p i) (s j) -> p (b i) s j", i=TOK_TILES, s=2),
         )
         gain_row = const.tile([P, KVR], BF16, name="gain_row")
-        nc.gpsimd.memset(gain_row[:], 0.0)
+        nc.vector.memset(gain_row[:], 0.0)
         nc.scalar.dma_start(
             out=gain_row[0:1, :], in_=kv_a_norm_w.rearrange("(o n) -> o n", o=1)
         )
@@ -116,8 +116,6 @@ def tile_deepseekmultiheadattention_pb_kernel(
         load_wb(1)
         load_wb(2)
 
-        minus_half = const.tile([P, 1], F32, name="minus_half")
-        nc.vector.memset(minus_half[:], -0.5)
         ones = const.tile([P, P], BF16, name="ones")
         nc.vector.memset(ones[:], 1.0)
         table_warmer = const.tile([P, 1], F32, name="table_warmer")
@@ -136,23 +134,32 @@ def tile_deepseekmultiheadattention_pb_kernel(
         make_identity(nc, ident_f32[:])
         ident_bf16 = const.tile([P, P], BF16, name="ident_bf16")
         make_identity(nc, ident_bf16[:])
-        angles = [P, 2, TOK_TILES, HALF_ROPE]
-        turns = const.tile(angles, F32, name="turns")
-        nc.vector.tensor_scalar_mul(out=turns[:, 0, :, 0], in0=pos[:], scalar1=1.0 / TWO_PI)
-        for step in range(5):
-            width = 2 ** step
+        turns = const.tile([P, TOK_TILES, HALF_ROPE], F32, name="turns")
+        for j in range(4):
             nc.vector.tensor_scalar_mul(
-                out=turns[:, 0, :, width : 2 * width],
-                in0=turns[:, 0, :, 0:width],
-                scalar1=ROPE_BASE ** (-width / HALF_ROPE),
+                out=turns[:, :, j], in0=pos[:], scalar1=ROPE_BASE ** (-j / HALF_ROPE) / TWO_PI
             )
-        nc.vector.tensor_scalar_add(out=turns[:, 1], in0=turns[:, 0], scalar1=0.25)
+        for first, width in ((4, 4), (8, 4), (12, 4), (16, 16)):
+            nc.vector.tensor_scalar_mul(
+                out=turns[:, :, first : first + width],
+                in0=turns[:, :, 0:width],
+                scalar1=ROPE_BASE ** (-first / HALF_ROPE),
+            )
+        angles = [P, 2, TOK_TILES, HALF_ROPE]
         whole = const.tile(angles, I32, name="whole")
-        nc.vector.tensor_copy(out=whole[:], in_=turns[:])
+        nc.vector.tensor_copy(out=whole[:, 0], in_=turns[:])
+        nc.vector.tensor_scalar_add(out=whole[:, 1], in0=turns[:], scalar1=0.25)
         phase = const.tile(angles, F32, name="phase")
-        nc.vector.tensor_tensor(out=phase[:], in0=turns[:], in1=whole[:], op=ALU.subtract)
+        nc.vector.tensor_tensor(
+            out=phase[:, 0], in0=turns[:], in1=whole[:, 0], op=ALU.subtract
+        )
+        nc.vector.scalar_tensor_tensor(
+            out=phase[:, 1], in0=turns[:], scalar=0.25, in1=whole[:, 1],
+            op0=ALU.add, op1=ALU.subtract,
+        )
         sin_cos = const.tile(angles, F32, name="sin_cos")
         nc.scalar.activation(out=sin_cos[:], in_=phase[:], func=ACT.Sin, scale=TWO_PI)
+        nc.scalar.activation(out=table_warmer[:], in_=table_warmer[:], func=ACT.Sqrt)
 
         ks_stage = [
             keep.tile([P, GROUP, TOK_TILES, NOPE + ROPE], F32, name="ks_stage%d" % b)
@@ -198,6 +205,9 @@ def tile_deepseekmultiheadattention_pb_kernel(
         def spread_gain():
             gain_ps = psum.tile([P, KVR], F32, tag="bank", name="gain_ps")
             nc.tensor.matmul(gain_ps[:], lhsT=ones[:], rhs=gain_row[:], start=True, stop=True)
+            return gain_ps
+
+        def keep_gain(gain_ps):
             nc.scalar.copy(out=gain[:], in_=gain_ps[:].rearrange("p (q t) -> p t q", t=PACK))
 
         def codes_and_scales(name, width):
@@ -264,6 +274,8 @@ def tile_deepseekmultiheadattention_pb_kernel(
             quantise(x_grouped[i][:], x_q[i])
 
         acc_of = {}
+        mean_sq_of = {}
+        rms_of = {}
         inv_rms_of = {}
 
         def project(i):
@@ -277,27 +289,36 @@ def tile_deepseekmultiheadattention_pb_kernel(
                 out=squares[:], in_=acc[:], func=ACT.Square,
                 scale=1.0 / math.sqrt(KVR), accum_out=mean_sq[:],
             )
-            shifted = work.tile([P, 1], F32, tag="shifted", bufs=4, name="shifted")
-            nc.gpsimd.tensor_scalar_add(out=shifted[:], in0=mean_sq[:], scalar1=EPS)
-            inv_rms = work.tile([P, 1], F32, tag="inv_rms", bufs=4, name="inv_rms")
-            nc.gpsimd.tensor_tensor(
-                out=inv_rms[:], in0=shifted[:], in1=minus_half[:], op=ALU.pow
-            )
             acc_of[i] = acc
+            mean_sq_of[i] = mean_sq
+
+        def root(i):
+            rms = work.tile([P, 1], F32, tag="rms", bufs=4, name="rms")
+            nc.scalar.activation(out=rms[:], in_=mean_sq_of[i][:], func=ACT.Sqrt, bias=EPS)
+            rms_of[i] = rms
+
+        def invert_rms(i):
+            inv_rms = work.tile([P, 1], F32, tag="inv_rms", bufs=4, name="inv_rms")
+            nc.vector.reciprocal(out=inv_rms[:], in_=rms_of[i][:])
             inv_rms_of[i] = inv_rms
 
-        def normalise(i):
+        def scale_cn(i):
             acc = acc_of[i]
+            inv_rms = inv_rms_of[i]
             cn = work.tile([P, PACK, P], BF16, tag="cn", bufs=4, name="cn")
             nc.vector.scalar_tensor_tensor(
                 out=cn[:],
                 in0=acc[:].rearrange("p (q t) -> p t q", t=PACK),
-                scalar=inv_rms_of[i][:, 0:1],
+                scalar=inv_rms[:, 0:1],
                 in1=gain[:],
                 op0=ALU.mult,
                 op1=ALU.mult,
             )
             cn_rows[i] = cn
+
+        def normalise(i):
+            invert_rms(i)
+            scale_cn(i)
 
         def transpose_cn(i):
             cn_t = psum.tile([P, PACK, P], BF16, tag="bank", name="cn_t")
@@ -323,13 +344,13 @@ def tile_deepseekmultiheadattention_pb_kernel(
             flat = grouped_columns(KVR)
             dst = flat.rearrange("p (c i t) -> p c t i", i=RUN, t=PACK)
             src = wc_raw[g][:].rearrange("p t (c i) -> p c t i", i=RUN)
-            middle = KVR // RUN // 2
-            nc.scalar.copy(out=dst[:, 0:middle], in_=src[:, 0:middle])
+            middle = KVR // RUN // 2 if g > 0 else 0
+            if middle:
+                nc.scalar.copy(out=dst[:, 0:middle], in_=src[:, 0:middle])
             nc.vector.tensor_copy(out=dst[:, middle:], in_=src[:, middle:])
             return flat
 
-        def regroup_wb(m, first, width, on_scalar):
-            flat = grouped_columns(GROUP * width)
+        def regroup_wb(m, first, width, flat, part, on_scalar):
             w = min(m, 2)
             head = GROUP * (m - wb_groups[w][0])
             heads = wb_raw[w][:].rearrange("p t (h f) -> p t h f", f=HEAD_COLS)
@@ -338,26 +359,35 @@ def tile_deepseekmultiheadattention_pb_kernel(
                 "p t h (c i) -> p h c t i", i=RUN
             )
             if on_scalar:
-                nc.scalar.copy(out=dst, in_=src)
+                nc.scalar.copy(out=dst[:, part], in_=src[:, part])
             else:
-                nc.vector.tensor_copy(out=dst, in_=src)
-            return flat
+                nc.vector.tensor_copy(out=dst[:, part], in_=src[:, part])
 
-        def v_half(m, half, share):
-            stage = work.tile([P, GROUP, HALF_TILES, VD], F32, tag="v_stage", bufs=4,
-                              name="v_stage")
-            for s in range(HALF_TILES):
+        v_stage_of = {}
+
+        def v_tiles(m, half, share, tiles):
+            if tiles[0] == 0:
+                v_stage_of[m, half] = work.tile(
+                    [P, GROUP, HALF_TILES, VD], F32, tag="v_stage", bufs=4, name="v_stage"
+                )
+            stage = v_stage_of[m, half]
+            for s in tiles:
                 i = HALF_TILES * half + s
                 kv = psum.tile([P, GROUP * VD], F32, tag="bank", name="kv")
                 mx(kv[:], cn_q[i], slice(0, P), wv_q[m], slice(0, GROUP * VD), True, True)
                 leave_psum(
                     s, share, stage[:, :, s, :], kv[:].rearrange("p (h d) -> p h d", h=GROUP)
                 )
+            if tiles[-1] < HALF_TILES - 1:
+                return
             nc.sync.dma_start(
                 out=v_view[:, GROUP * m : GROUP * (m + 1),
                            HALF_TILES * half : HALF_TILES * (half + 1), :],
                 in_=stage[:],
             )
+
+        def v_half(m, half, share):
+            v_tiles(m, half, share, range(HALF_TILES))
 
         def v_pair(m, pair):
             stage = work.tile([P, PAIR, TOK_TILES, VD], F32, tag="v_stage", bufs=4,
@@ -396,11 +426,15 @@ def tile_deepseekmultiheadattention_pb_kernel(
 
         flat_of = {}
 
-        def regroup_v(m, on_scalar=False):
-            flat_of[m, 0] = regroup_wb(m, NOPE, VD, on_scalar)
+        def regroup_v(m, part=slice(0, GROUP), on_scalar=False):
+            if (m, 0) not in flat_of:
+                flat_of[m, 0] = grouped_columns(GROUP * VD)
+            regroup_wb(m, NOPE, VD, flat_of[m, 0], part, on_scalar)
 
-        def regroup_k(m, on_scalar=False):
-            flat_of[m, 1] = regroup_wb(m, 0, NOPE, on_scalar)
+        def regroup_k(m, part=slice(0, GROUP), on_scalar=False):
+            if (m, 1) not in flat_of:
+                flat_of[m, 1] = grouped_columns(GROUP * NOPE)
+            regroup_wb(m, 0, NOPE, flat_of[m, 1], part, on_scalar)
 
         def quantise_v(m):
             quantise(flat_of[m, 0], wv_q[m])
@@ -427,55 +461,69 @@ def tile_deepseekmultiheadattention_pb_kernel(
                 quantise_k(u // 2)
 
         flats = {}
-        multiply_k_pe()
         for g in range(X_PASSES):
             flats[g] = regroup_wc(g)
-            if g == 0:
-                rotate_k_pe()
-            else:
+            if g > 0:
                 quantise(flats[g - 1], wc_q[g - 1])
         quantise(flats[X_PASSES - 1], wc_q[X_PASSES - 1])
-        fill_rope(0, 0)
+        gain_ps = spread_gain()
+        multiply_k_pe()
         for i in range(HALF_TILES):
             transpose_x(i)
         quantise_x(0)
-        fill_rope(1, 0)
+        rotate_k_pe()
         quantise_x(1)
+        fill_rope(0, 0)
         quantise_x(2)
-        regroup_v(0)
         quantise_x(3)
-        spread_gain()
-        for i in range(HALF_TILES):
-            project(i)
-            if i == 0:
-                regroup_k(0, True)
-        normalise(0)
+        keep_gain(gain_ps)
+        project(0)
+        regroup_v(0, slice(0, 3))
+        regroup_v(0, slice(3, 4), True)
+        root(0)
+        project(1)
+        project(2)
+        root(1)
+        project(3)
+        root(2)
+        root(3)
+        invert_rms(0)
         quantise_v(0)
-        normalise(1)
-        normalise(2)
-        normalise(3)
+        scale_cn(0)
+        invert_rms(1)
+        invert_rms(2)
+        scale_cn(1)
+        scale_cn(2)
+        invert_rms(3)
+        scale_cn(3)
         for i in range(HALF_TILES):
             transpose_cn(i)
         for i in range(HALF_TILES):
             quantise_cn(i)
-        for u in range(8):
-            if u + 1 < 8:
+        for u in range(9):
+            if 0 < u < 7:
                 quantise_unit(u + 1)
-            unit(u, 0, 2 if u == 0 else 4)
-            if 3 <= u < 7:
-                normalise(u + 1)
-            if u + 2 < 8:
+            if u < 8:
+                unit(u, 0, 2 if u == 0 else 4)
+            if u == 0:
+                regroup_k(0)
+                quantise_k(0)
+            if 4 <= u < 8:
+                normalise(u)
+            if u == 0:
+                fill_rope(1, 0)
+            if u < 6:
                 regroup_unit(u + 2)
             if u < 4:
                 transpose_x(u + 4)
             if 1 <= u < 5:
                 quantise_x(u + 3)
-            if 2 <= u < 6:
-                project(u + 2)
-            if 4 <= u < 8:
-                transpose_cn(u + 0)
-            if 4 <= u < 8:
-                quantise_cn(u + 0)
+            if 3 <= u < 7:
+                project(u + 1)
+                root(u + 1)
+            if u >= 5:
+                transpose_cn(u - 1)
+                quantise_cn(u - 1)
         fill_rope(0, 1)
         fill_rope(1, 1)
         for u in range(8):

@@ -31,7 +31,7 @@ GROUPS = H // GROUP
 PAIR = 2
 HALVES = 2
 HALF_TILES = TOK_TILES // HALVES
-HALF_GROUPS = 4
+HALF_GROUPS = 3
 
 TWO_PI = 2.0 * math.pi
 
@@ -500,31 +500,52 @@ def tile_deepseekmultiheadattention_pb_kernel(
             transpose_cn(i)
         for i in range(HALF_TILES):
             quantise_cn(i)
-        for u in range(9):
-            if 0 < u < 7:
+        def pair_of_second_half(n):
+            return range(HALF_TILES + 2 * n, HALF_TILES + 2 * n + 2) if 0 <= n < 2 else ()
+
+        units = 2 * HALF_GROUPS
+        for u in range(units + 1):
+            if 0 < u < units - 1:
                 quantise_unit(u + 1)
-            if u < 8:
+            if u < units:
                 unit(u, 0, 2 if u == 0 else 4)
             if u == 0:
                 regroup_k(0)
                 quantise_k(0)
-            if 4 <= u < 8:
-                normalise(u)
+            for i in pair_of_second_half(u - 4):
+                normalise(i)
             if u == 0:
                 fill_rope(1, 0)
-            if u < 6:
+            if u < units - 2:
                 regroup_unit(u + 2)
-            if u < 4:
-                transpose_x(u + 4)
-            if 1 <= u < 5:
-                quantise_x(u + 3)
-            if 3 <= u < 7:
-                project(u + 1)
-                root(u + 1)
-            if u >= 5:
-                transpose_cn(u - 1)
-                quantise_cn(u - 1)
-        fill_rope(0, 1)
-        fill_rope(1, 1)
-        for u in range(8):
+            for i in pair_of_second_half(u):
+                transpose_x(i)
+            for i in pair_of_second_half(u - 1):
+                quantise_x(i)
+            for i in pair_of_second_half(u - 3):
+                project(i)
+                root(i)
+            for i in pair_of_second_half(u - 5):
+                transpose_cn(i)
+            for i in pair_of_second_half(u - 5):
+                quantise_cn(i)
+        for u in range(units):
+            if u % 2 == 1 and u < 4:
+                fill_rope(u // 2, 1)
             unit(u, 1, 2)
+            if u == 1:
+                regroup_v(HALF_GROUPS)
+                regroup_k(HALF_GROUPS)
+            if u == 2:
+                quantise_v(HALF_GROUPS)
+                quantise_k(HALF_GROUPS)
+        for m in range(HALF_GROUPS, GROUPS):
+            v_pair(m, 0)
+            if m + 1 < GROUPS:
+                regroup_v(m + 1)
+                regroup_k(m + 1)
+            v_pair(m, 1)
+            if m + 1 < GROUPS:
+                quantise_v(m + 1)
+                quantise_k(m + 1)
+            k_tiles(m, 0, TOK_TILES, 2)

@@ -54,24 +54,13 @@ def tile_deepseekmultiheadattention_pb_kernel(
         ks_view = out_0.rearrange("b h (p i) d -> p (b h) i d", i=TOK_TILES)
         v_view = out_1.rearrange("b h (p i) d -> p (b h) i d", i=TOK_TILES)
 
-        kp = const.tile([P, TOK_TILES, 2, HALF_ROPE], BF16, name="kp")
-        nc.scalar.dma_start(
-            out=kp[:],
-            in_=k_pe.rearrange("b (p i) (s j) -> p (b i) s j", i=TOK_TILES, s=2),
-        )
-        gain_row = const.tile([P, KVR], BF16, name="gain_row")
-        nc.vector.memset(gain_row[:], 0.0)
-        nc.scalar.dma_start(
-            out=gain_row[0:1, :], in_=kv_a_norm_w.rearrange("(o n) -> o n", o=1)
-        )
-
 
         x_single = [keep.tile([P, D], BF16, name="x_single%d" % i) for i in range(HALF_TILES)]
         x_pairs = [keep.tile([P, 2, D], BF16, name="x_pair%d" % j) for j in range(2)]
         wc_raw = [
             keep.tile([P, PACK, KVR], BF16, name="wc_raw%d" % g) for g in range(X_PASSES)
         ]
-        wb_groups = [(0, 1), (1, 1), (2, 2)]
+        wb_groups = [(0, 1), (1, GROUPS - 1)]
         wb_raw = [
             keep.tile([P, PACK, n * GROUP * HEAD_COLS], BF16, name="wb_raw%d" % first)
             for first, n in wb_groups
@@ -103,6 +92,27 @@ def tile_deepseekmultiheadattention_pb_kernel(
             nc.sync.dma_start(out=x_single[i][:], in_=x_view[:, i, :])
 
         load_wc(0)
+        table_warmer = const.tile([P, 1], F32, name="table_warmer")
+        nc.vector.memset(table_warmer[:], 0.0)
+        nc.scalar.activation(out=table_warmer[:], in_=table_warmer[:], func=ACT.Sin)
+        pos = const.tile([P, TOK_TILES], F32, name="pos")
+        nc.gpsimd.iota(
+            pos[:],
+            pattern=[[1, TOK_TILES]],
+            base=0,
+            channel_multiplier=TOK_TILES,
+            allow_small_or_imprecise_dtypes=True,
+        )
+        kp = const.tile([P, TOK_TILES, 2, HALF_ROPE], BF16, name="kp")
+        nc.scalar.dma_start(
+            out=kp[:],
+            in_=k_pe.rearrange("b (p i) (s j) -> p (b i) s j", i=TOK_TILES, s=2),
+        )
+        gain_row = const.tile([P, KVR], BF16, name="gain_row")
+        nc.gpsimd.memset(gain_row[:], 0.0)
+        nc.scalar.dma_start(
+            out=gain_row[0:1, :], in_=kv_a_norm_w.rearrange("(o n) -> o n", o=1)
+        )
         load_wc(1)
         load_wc(2)
         load_wc(3)
@@ -114,22 +124,8 @@ def tile_deepseekmultiheadattention_pb_kernel(
         load_x_pair(0)
         load_x_pair(1)
         load_wb(1)
-        load_wb(2)
 
-        ones = const.tile([P, P], BF16, name="ones")
-        nc.vector.memset(ones[:], 1.0)
-        table_warmer = const.tile([P, 1], F32, name="table_warmer")
-        nc.vector.memset(table_warmer[:], 0.0)
-        nc.scalar.activation(out=table_warmer[:], in_=table_warmer[:], func=ACT.Sin)
 
-        pos = const.tile([P, TOK_TILES], F32, name="pos")
-        nc.gpsimd.iota(
-            pos[:],
-            pattern=[[1, TOK_TILES]],
-            base=0,
-            channel_multiplier=TOK_TILES,
-            allow_small_or_imprecise_dtypes=True,
-        )
         ident_f32 = const.tile([P, P], F32, name="ident_f32")
         make_identity(nc, ident_f32[:])
         ident_bf16 = const.tile([P, P], BF16, name="ident_bf16")
@@ -160,6 +156,9 @@ def tile_deepseekmultiheadattention_pb_kernel(
         sin_cos = const.tile(angles, F32, name="sin_cos")
         nc.scalar.activation(out=sin_cos[:], in_=phase[:], func=ACT.Sin, scale=TWO_PI)
         nc.scalar.activation(out=table_warmer[:], in_=table_warmer[:], func=ACT.Sqrt)
+
+        ones = const.tile([P, P], BF16, name="ones")
+        nc.vector.memset(ones[:], 1.0)
 
         ks_stage = [
             keep.tile([P, GROUP, TOK_TILES, NOPE + ROPE], F32, name="ks_stage%d" % b)
@@ -351,7 +350,7 @@ def tile_deepseekmultiheadattention_pb_kernel(
             return flat
 
         def regroup_wb(m, first, width, flat, part, on_scalar):
-            w = min(m, 2)
+            w = min(m, 1)
             head = GROUP * (m - wb_groups[w][0])
             heads = wb_raw[w][:].rearrange("p t (h f) -> p t h f", f=HEAD_COLS)
             dst = flat.rearrange("p (h c i t) -> p h c t i", h=GROUP, i=RUN, t=PACK)
@@ -466,36 +465,30 @@ def tile_deepseekmultiheadattention_pb_kernel(
             if g > 0:
                 quantise(flats[g - 1], wc_q[g - 1])
         quantise(flats[X_PASSES - 1], wc_q[X_PASSES - 1])
-        gain_ps = spread_gain()
         multiply_k_pe()
         for i in range(HALF_TILES):
             transpose_x(i)
         quantise_x(0)
         rotate_k_pe()
         quantise_x(1)
-        fill_rope(0, 0)
         quantise_x(2)
+        fill_rope(0, 0)
         quantise_x(3)
-        keep_gain(gain_ps)
-        project(0)
-        regroup_v(0, slice(0, 3))
         regroup_v(0, slice(3, 4), True)
+        project(0)
         root(0)
-        project(1)
-        project(2)
-        root(1)
-        project(3)
-        root(2)
-        root(3)
+        gain_ps = spread_gain()
+        keep_gain(gain_ps)
+        regroup_v(0, slice(0, 3))
+        for i in range(1, HALF_TILES):
+            project(i)
+            root(i)
         invert_rms(0)
-        quantise_v(0)
         scale_cn(0)
-        invert_rms(1)
-        invert_rms(2)
-        scale_cn(1)
-        scale_cn(2)
-        invert_rms(3)
-        scale_cn(3)
+        quantise_v(0)
+        for i in range(1, HALF_TILES):
+            invert_rms(i)
+            scale_cn(i)
         for i in range(HALF_TILES):
             transpose_cn(i)
         for i in range(HALF_TILES):

@@ -31,7 +31,7 @@ GROUPS = H // GROUP
 PAIR = 2
 HALVES = 2
 HALF_TILES = TOK_TILES // HALVES
-HALF_GROUPS = 3
+HALF_GROUPS = 4
 
 TWO_PI = 2.0 * math.pi
 
@@ -54,13 +54,24 @@ def tile_deepseekmultiheadattention_pb_kernel(
         ks_view = out_0.rearrange("b h (p i) d -> p (b h) i d", i=TOK_TILES)
         v_view = out_1.rearrange("b h (p i) d -> p (b h) i d", i=TOK_TILES)
 
+        kp = const.tile([P, TOK_TILES, 2, HALF_ROPE], BF16, name="kp")
+        nc.scalar.dma_start(
+            out=kp[:],
+            in_=k_pe.rearrange("b (p i) (s j) -> p (b i) s j", i=TOK_TILES, s=2),
+        )
+        gain_row = const.tile([P, KVR], BF16, name="gain_row")
+        nc.gpsimd.memset(gain_row[:], 0.0)
+        nc.scalar.dma_start(
+            out=gain_row[0:1, :], in_=kv_a_norm_w.rearrange("(o n) -> o n", o=1)
+        )
+
 
         x_single = [keep.tile([P, D], BF16, name="x_single%d" % i) for i in range(HALF_TILES)]
         x_pairs = [keep.tile([P, 2, D], BF16, name="x_pair%d" % j) for j in range(2)]
         wc_raw = [
             keep.tile([P, PACK, KVR], BF16, name="wc_raw%d" % g) for g in range(X_PASSES)
         ]
-        wb_groups = [(0, 1), (1, GROUPS - 1)]
+        wb_groups = [(0, 1), (1, 1), (2, 2)]
         wb_raw = [
             keep.tile([P, PACK, n * GROUP * HEAD_COLS], BF16, name="wb_raw%d" % first)
             for first, n in wb_groups
@@ -92,27 +103,6 @@ def tile_deepseekmultiheadattention_pb_kernel(
             nc.sync.dma_start(out=x_single[i][:], in_=x_view[:, i, :])
 
         load_wc(0)
-        table_warmer = const.tile([P, 1], F32, name="table_warmer")
-        nc.vector.memset(table_warmer[:], 0.0)
-        nc.scalar.activation(out=table_warmer[:], in_=table_warmer[:], func=ACT.Sin)
-        pos = const.tile([P, TOK_TILES], F32, name="pos")
-        nc.gpsimd.iota(
-            pos[:],
-            pattern=[[1, TOK_TILES]],
-            base=0,
-            channel_multiplier=TOK_TILES,
-            allow_small_or_imprecise_dtypes=True,
-        )
-        kp = const.tile([P, TOK_TILES, 2, HALF_ROPE], BF16, name="kp")
-        nc.scalar.dma_start(
-            out=kp[:],
-            in_=k_pe.rearrange("b (p i) (s j) -> p (b i) s j", i=TOK_TILES, s=2),
-        )
-        gain_row = const.tile([P, KVR], BF16, name="gain_row")
-        nc.gpsimd.memset(gain_row[:], 0.0)
-        nc.scalar.dma_start(
-            out=gain_row[0:1, :], in_=kv_a_norm_w.rearrange("(o n) -> o n", o=1)
-        )
         load_wc(1)
         load_wc(2)
         load_wc(3)
@@ -124,8 +114,22 @@ def tile_deepseekmultiheadattention_pb_kernel(
         load_x_pair(0)
         load_x_pair(1)
         load_wb(1)
+        load_wb(2)
 
+        ones = const.tile([P, P], BF16, name="ones")
+        nc.vector.memset(ones[:], 1.0)
+        table_warmer = const.tile([P, 1], F32, name="table_warmer")
+        nc.vector.memset(table_warmer[:], 0.0)
+        nc.scalar.activation(out=table_warmer[:], in_=table_warmer[:], func=ACT.Sin)
 
+        pos = const.tile([P, TOK_TILES], F32, name="pos")
+        nc.gpsimd.iota(
+            pos[:],
+            pattern=[[1, TOK_TILES]],
+            base=0,
+            channel_multiplier=TOK_TILES,
+            allow_small_or_imprecise_dtypes=True,
+        )
         ident_f32 = const.tile([P, P], F32, name="ident_f32")
         make_identity(nc, ident_f32[:])
         ident_bf16 = const.tile([P, P], BF16, name="ident_bf16")
@@ -156,9 +160,6 @@ def tile_deepseekmultiheadattention_pb_kernel(
         sin_cos = const.tile(angles, F32, name="sin_cos")
         nc.scalar.activation(out=sin_cos[:], in_=phase[:], func=ACT.Sin, scale=TWO_PI)
         nc.scalar.activation(out=table_warmer[:], in_=table_warmer[:], func=ACT.Sqrt)
-
-        ones = const.tile([P, P], BF16, name="ones")
-        nc.vector.memset(ones[:], 1.0)
 
         ks_stage = [
             keep.tile([P, GROUP, TOK_TILES, NOPE + ROPE], F32, name="ks_stage%d" % b)
@@ -350,7 +351,7 @@ def tile_deepseekmultiheadattention_pb_kernel(
             return flat
 
         def regroup_wb(m, first, width, flat, part, on_scalar):
-            w = min(m, 1)
+            w = min(m, 2)
             head = GROUP * (m - wb_groups[w][0])
             heads = wb_raw[w][:].rearrange("p t (h f) -> p t h f", f=HEAD_COLS)
             dst = flat.rearrange("p (h c i t) -> p h c t i", h=GROUP, i=RUN, t=PACK)
@@ -442,22 +443,25 @@ def tile_deepseekmultiheadattention_pb_kernel(
             quantise(flat_of[m, 1], wk_q[m])
 
         def unit(u, half, share):
-            if u % 2 == 0:
-                v_half(u // 2, half, share)
+            kind, m = u
+            if kind == "v":
+                v_half(m, half, share)
             else:
-                k_tiles(u // 2, HALF_TILES * half, HALF_TILES, share)
+                k_tiles(m, HALF_TILES * half, HALF_TILES, share)
 
         def regroup_unit(u):
-            if u % 2 == 0:
-                regroup_v(u // 2)
+            kind, m = u
+            if kind == "v":
+                regroup_v(m)
             else:
-                regroup_k(u // 2)
+                regroup_k(m)
 
         def quantise_unit(u):
-            if u % 2 == 0:
-                quantise_v(u // 2)
+            kind, m = u
+            if kind == "v":
+                quantise_v(m)
             else:
-                quantise_k(u // 2)
+                quantise_k(m)
 
         flats = {}
         for g in range(X_PASSES):
@@ -466,79 +470,99 @@ def tile_deepseekmultiheadattention_pb_kernel(
                 quantise(flats[g - 1], wc_q[g - 1])
         quantise(flats[X_PASSES - 1], wc_q[X_PASSES - 1])
         multiply_k_pe()
-        for i in range(HALF_TILES):
-            transpose_x(i)
+        transpose_x(0)
+        transpose_x(1)
+        transpose_x(2)
+        transpose_x(3)
         quantise_x(0)
         rotate_k_pe()
         quantise_x(1)
         quantise_x(2)
         fill_rope(0, 0)
         quantise_x(3)
-        regroup_v(0, slice(3, 4), True)
+        regroup_k(0)
         project(0)
         root(0)
         gain_ps = spread_gain()
         keep_gain(gain_ps)
-        regroup_v(0, slice(0, 3))
-        for i in range(1, HALF_TILES):
-            project(i)
-            root(i)
+        project(1)
+        root(1)
+        project(2)
+        root(2)
+        project(3)
+        root(3)
         invert_rms(0)
         scale_cn(0)
+        quantise_k(0)
+        normalise(1)
+        normalise(2)
+        normalise(3)
+        transpose_cn(0)
+        transpose_cn(1)
+        transpose_cn(2)
+        transpose_cn(3)
+        quantise_cn(0)
+        quantise_cn(1)
+        quantise_cn(2)
+        quantise_cn(3)
+        unit(("k", 0), 0, 9)
+        regroup_k(1)
+        fill_rope(1, 0)
+        quantise_k(1)
+        transpose_x(4)
+        unit(("k", 1), 0, 9)
+        regroup_v(0)
+        transpose_x(5)
         quantise_v(0)
-        for i in range(1, HALF_TILES):
-            invert_rms(i)
-            scale_cn(i)
-        for i in range(HALF_TILES):
-            transpose_cn(i)
-        for i in range(HALF_TILES):
-            quantise_cn(i)
-        def pair_of_second_half(n):
-            return range(HALF_TILES + 2 * n, HALF_TILES + 2 * n + 2) if 0 <= n < 2 else ()
-
-        units = 2 * HALF_GROUPS
-        for u in range(units + 1):
-            if 0 < u < units - 1:
-                quantise_unit(u + 1)
-            if u < units:
-                unit(u, 0, 2 if u == 0 else 4)
-            if u == 0:
-                regroup_k(0)
-                quantise_k(0)
-            for i in pair_of_second_half(u - 4):
-                normalise(i)
-            if u == 0:
-                fill_rope(1, 0)
-            if u < units - 2:
-                regroup_unit(u + 2)
-            for i in pair_of_second_half(u):
-                transpose_x(i)
-            for i in pair_of_second_half(u - 1):
-                quantise_x(i)
-            for i in pair_of_second_half(u - 3):
-                project(i)
-                root(i)
-            for i in pair_of_second_half(u - 5):
-                transpose_cn(i)
-            for i in pair_of_second_half(u - 5):
-                quantise_cn(i)
-        for u in range(units):
-            if u % 2 == 1 and u < 4:
-                fill_rope(u // 2, 1)
-            unit(u, 1, 2)
-            if u == 1:
-                regroup_v(HALF_GROUPS)
-                regroup_k(HALF_GROUPS)
-            if u == 2:
-                quantise_v(HALF_GROUPS)
-                quantise_k(HALF_GROUPS)
-        for m in range(HALF_GROUPS, GROUPS):
-            v_pair(m, 0)
-            if m + 1 < GROUPS:
-                regroup_v(m + 1)
-                regroup_k(m + 1)
-            v_pair(m, 1)
-            if m + 1 < GROUPS:
-                quantise_v(m + 1)
-                quantise_k(m + 1)
-            k_tiles(m, 0, TOK_TILES, 2)
+        quantise_x(4)
+        unit(("v", 0), 0, 2)
+        regroup_k(2)
+        quantise_k(2)
+        transpose_x(6)
+        transpose_x(7)
+        unit(("k", 2), 0, 9)
+        quantise_x(5)
+        regroup_k(3)
+        quantise_k(3)
+        project(4)
+        root(4)
+        project(5)
+        root(5)
+        unit(("k", 3), 0, 9)
+        quantise_x(6)
+        regroup_v(1)
+        quantise_x(7)
+        normalise(4)
+        normalise(5)
+        quantise_v(1)
+        fill_rope(0, 1)
+        project(6)
+        root(6)
+        project(7)
+        root(7)
+        normalise(6)
+        unit(("v", 1), 0, 2)
+        normalise(7)
+        transpose_cn(4)
+        transpose_cn(5)
+        transpose_cn(6)
+        transpose_cn(7)
+        quantise_cn(4)
+        quantise_cn(5)
+        quantise_cn(6)
+        quantise_cn(7)
+        unit(("k", 0), 1, 2)
+        unit(("v", 0), 1, 2)
+        fill_rope(1, 1)
+        unit(("k", 1), 1, 2)
+        regroup_v(2)
+        unit(("k", 2), 1, 2)
+        quantise_v(2)
+        unit(("v", 1), 1, 2)
+        regroup_v(3)
+        unit(("k", 3), 1, 2)
+        quantise_v(3)
+        v_pair(2, 0)
+        v_pair(2, 1)
+        v_pair(3, 0)
+        v_pair(3, 1)

@@ -59,8 +59,16 @@ def tile_deepseekmultiheadattention_pb_kernel(
             out=kp[:],
             in_=k_pe.rearrange("b (p i) (s j) -> p (b i) s j", i=TOK_TILES, s=2),
         )
+        pos = const.tile([P, TOK_TILES], F32, name="pos")
+        nc.gpsimd.iota(
+            pos[:],
+            pattern=[[1, TOK_TILES]],
+            base=0,
+            channel_multiplier=TOK_TILES,
+            allow_small_or_imprecise_dtypes=True,
+        )
         gain_row = const.tile([P, KVR], BF16, name="gain_row")
-        nc.gpsimd.memset(gain_row[:], 0.0)
+        nc.vector.memset(gain_row[:].bitcast(I32), 0)
         nc.scalar.dma_start(
             out=gain_row[0:1, :], in_=kv_a_norm_w.rearrange("(o n) -> o n", o=1)
         )
@@ -71,7 +79,7 @@ def tile_deepseekmultiheadattention_pb_kernel(
         wc_raw = [
             keep.tile([P, PACK, KVR], BF16, name="wc_raw%d" % g) for g in range(X_PASSES)
         ]
-        wb_groups = [(0, 1), (1, 1), (2, 2)]
+        wb_groups = [(0, 2), (2, 2)]
         wb_raw = [
             keep.tile([P, PACK, n * GROUP * HEAD_COLS], BF16, name="wb_raw%d" % first)
             for first, n in wb_groups
@@ -114,7 +122,6 @@ def tile_deepseekmultiheadattention_pb_kernel(
         load_x_pair(0)
         load_x_pair(1)
         load_wb(1)
-        load_wb(2)
 
         ones = const.tile([P, P], BF16, name="ones")
         nc.vector.memset(ones[:], 1.0)
@@ -122,14 +129,6 @@ def tile_deepseekmultiheadattention_pb_kernel(
         nc.vector.memset(table_warmer[:], 0.0)
         nc.scalar.activation(out=table_warmer[:], in_=table_warmer[:], func=ACT.Sin)
 
-        pos = const.tile([P, TOK_TILES], F32, name="pos")
-        nc.gpsimd.iota(
-            pos[:],
-            pattern=[[1, TOK_TILES]],
-            base=0,
-            channel_multiplier=TOK_TILES,
-            allow_small_or_imprecise_dtypes=True,
-        )
         ident_f32 = const.tile([P, P], F32, name="ident_f32")
         make_identity(nc, ident_f32[:])
         ident_bf16 = const.tile([P, P], BF16, name="ident_bf16")
@@ -351,7 +350,7 @@ def tile_deepseekmultiheadattention_pb_kernel(
             return flat
 
         def regroup_wb(m, first, width, flat, part, on_scalar):
-            w = min(m, 2)
+            w = m // 2
             head = GROUP * (m - wb_groups[w][0])
             heads = wb_raw[w][:].rearrange("p t (h f) -> p t h f", f=HEAD_COLS)
             dst = flat.rearrange("p (h c i t) -> p h c t i", h=GROUP, i=RUN, t=PACK)
@@ -470,21 +469,20 @@ def tile_deepseekmultiheadattention_pb_kernel(
                 quantise(flats[g - 1], wc_q[g - 1])
         quantise(flats[X_PASSES - 1], wc_q[X_PASSES - 1])
         multiply_k_pe()
+        gain_ps = spread_gain()
         transpose_x(0)
         transpose_x(1)
         transpose_x(2)
         transpose_x(3)
+        keep_gain(gain_ps)
         quantise_x(0)
         rotate_k_pe()
         quantise_x(1)
         quantise_x(2)
         fill_rope(0, 0)
         quantise_x(3)
-        regroup_k(0)
         project(0)
         root(0)
-        gain_ps = spread_gain()
-        keep_gain(gain_ps)
         project(1)
         root(1)
         project(2)
@@ -493,6 +491,7 @@ def tile_deepseekmultiheadattention_pb_kernel(
         root(3)
         invert_rms(0)
         scale_cn(0)
+        regroup_k(0)
         quantise_k(0)
         normalise(1)
         normalise(2)
@@ -535,7 +534,6 @@ def tile_deepseekmultiheadattention_pb_kernel(
         normalise(4)
         normalise(5)
         quantise_v(1)
-        fill_rope(0, 1)
         project(6)
         root(6)
         project(7)
@@ -545,10 +543,11 @@ def tile_deepseekmultiheadattention_pb_kernel(
         normalise(7)
         transpose_cn(4)
         transpose_cn(5)
-        transpose_cn(6)
-        transpose_cn(7)
         quantise_cn(4)
         quantise_cn(5)
+        transpose_cn(6)
+        transpose_cn(7)
+        fill_rope(0, 1)
         quantise_cn(6)
         quantise_cn(7)
         unit(("k", 0), 1, 2)

import math
from contextlib import ExitStack

import concourse.mybir as mybir
from concourse.masks import make_identity

F32 = mybir.dt.float32
BF16 = mybir.dt.bfloat16
I32 = mybir.dt.int32
U32 = mybir.dt.uint32
U8 = mybir.dt.uint8
FP8X4 = mybir.dt.float8_e4m3fn_x4
ALU = mybir.AluOpType
ACT = mybir.ActivationFunctionType

P = 128
PACK = 4
K_PASS = P * PACK
RUN = 4

T, D, KVR, H, NOPE, VD, ROPE = 1024, 2048, 512, 16, 64, 128, 64
HALF_ROPE = ROPE // 2
ROPE_BASE = 10000.0
EPS = 2.0 ** -23

TOK_TILES = T // P
X_PASSES = D // K_PASS
HEAD_COLS = NOPE + VD
GROUP = 4
GROUPS = H // GROUP
PAIR = 2
HALVES = 2
HALF_TILES = TOK_TILES // HALVES
HALF_GROUPS = 4

TWO_PI = 2.0 * math.pi

FLOPS = 2 * T * D * KVR + 2 * T * KVR * H * HEAD_COLS


def tile_deepseekmultiheadattention_pb_kernel(
    tc, x, wkv_c, kv_a_norm_w, wkv_b, k_pe, out_0, out_1
):
    nc = tc.nc
    with ExitStack() as ctx:
        const = ctx.enter_context(tc.tile_pool(name="const", bufs=1))
        keep = ctx.enter_context(tc.tile_pool(name="keep", bufs=1))
        work = ctx.enter_context(tc.tile_pool(name="work", bufs=2))
        psum = ctx.enter_context(tc.psum_pool(name="psum", bufs=8))
        ctx.enter_context(tc.manual_schedule())

        x_view = x.rearrange("b (p i) k -> p (b i) k", i=TOK_TILES)
        wb_view = wkv_b.rearrange("(p t) n -> p t n", t=PACK)
        ks_view = out_0.rearrange("b h (p i) d -> p (b h) i d", i=TOK_TILES)
        v_view = out_1.rearrange("b h (p i) d -> p (b h) i d", i=TOK_TILES)

        kp = const.tile([P, TOK_TILES, 2, HALF_ROPE], BF16, name="kp")
        nc.scalar.dma_start(
            out=kp[:],
            in_=k_pe.rearrange("b (p i) (s j) -> p (b i) s j", i=TOK_TILES, s=2),
        )
        pos = const.tile([P, TOK_TILES], F32, name="pos")
        nc.gpsimd.iota(
            pos[:],
            pattern=[[1, TOK_TILES]],
            base=0,
            channel_multiplier=TOK_TILES,
            allow_small_or_imprecise_dtypes=True,
        )
        gain_row = const.tile([P, KVR], BF16, name="gain_row")
        nc.vector.memset(gain_row[:].bitcast(I32), 0)
        nc.scalar.dma_start(
            out=gain_row[0:1, :], in_=kv_a_norm_w.rearrange("(o n) -> o n", o=1)
        )


        x_single = [keep.tile([P, D], BF16, name="x_single%d" % i) for i in range(HALF_TILES)]
        x_pairs = [keep.tile([P, 2, D], BF16, name="x_pair%d" % j) for j in range(2)]
        wc_raw = [
            keep.tile([P, PACK, KVR], BF16, name="wc_raw%d" % g) for g in range(X_PASSES)
        ]
        wb_groups = [(0, 2), (2, 2)]
        wb_raw = [
            keep.tile([P, PACK, n * GROUP * HEAD_COLS], BF16, name="wb_raw%d" % first)
            for first, n in wb_groups
        ]

        def load_wb(w):
            first, n = wb_groups[w]
            cols = slice(GROUP * HEAD_COLS * first, GROUP * HEAD_COLS * (first + n))
            nc.sync.dma_start(out=wb_raw[w][:], in_=wb_view[:, :, cols])

        def load_x_pair(j):
            first = HALF_TILES + 2 * j
            nc.sync.dma_start(out=x_pairs[j][:], in_=x_view[:, first : first + 2, :])

        def x_rows(i):
            if i < HALF_TILES:
                return x_single[i][:]
            return x_pairs[(i - HALF_TILES) // 2][:, i % 2, :]

        def load_wc(g):
            nc.sync.dma_start(
                out=wc_raw[g][:],
                in_=wkv_c[K_PASS * g : K_PASS * (g + 1), :].rearrange(
                    "(q t) c -> q t c", t=PACK
                ),
            )

        def load_x(i):
            nc.sync.dma_start(out=x_single[i][:], in_=x_view[:, i, :])

        load_wc(0)
        load_wc(1)
        load_wc(2)
        load_wc(3)
        load_x(0)
        load_x(1)
        load_x(2)
        load_x(3)
        load_wb(0)
        load_x_pair(0)
        load_x_pair(1)
        load_wb(1)

        ones = const.tile([P, P], BF16, name="ones")
        nc.vector.memset(ones[:], 1.0)
        table_warmer = const.tile([P, 1], F32, name="table_warmer")
        nc.vector.memset(table_warmer[:], 0.0)
        nc.scalar.activation(out=table_warmer[:], in_=table_warmer[:], func=ACT.Sin)

        ident_f32 = const.tile([P, P], F32, name="ident_f32")
        make_identity(nc, ident_f32[:])
        ident_bf16 = const.tile([P, P], BF16, name="ident_bf16")
        make_identity(nc, ident_bf16[:])
        turns = const.tile([P, TOK_TILES, HALF_ROPE], F32, name="turns")
        for j in range(4):
            nc.vector.tensor_scalar_mul(
                out=turns[:, :, j], in0=pos[:], scalar1=ROPE_BASE ** (-j / HALF_ROPE) / TWO_PI
            )
        for first, width in ((4, 4), (8, 4), (12, 4), (16, 16)):
            nc.vector.tensor_scalar_mul(
                out=turns[:, :, first : first + width],
                in0=turns[:, :, 0:width],
                scalar1=ROPE_BASE ** (-first / HALF_ROPE),
            )
        angles = [P, 2, TOK_TILES, HALF_ROPE]
        whole = const.tile(angles, I32, name="whole")
        nc.vector.tensor_copy(out=whole[:, 0], in_=turns[:])
        nc.vector.tensor_scalar_add(out=whole[:, 1], in0=turns[:], scalar1=0.25)
        phase = const.tile(angles, F32, name="phase")
        nc.vector.tensor_tensor(
            out=phase[:, 0], in0=turns[:], in1=whole[:, 0], op=ALU.subtract
        )
        nc.vector.scalar_tensor_tensor(
            out=phase[:, 1], in0=turns[:], scalar=0.25, in1=whole[:, 1],
            op0=ALU.add, op1=ALU.subtract,
        )
        sin_cos = const.tile(angles, F32, name="sin_cos")
        nc.scalar.activation(out=sin_cos[:], in_=phase[:], func=ACT.Sin, scale=TWO_PI)
        nc.scalar.activation(out=table_warmer[:], in_=table_warmer[:], func=ACT.Sqrt)

        ks_stage = [
            keep.tile([P, GROUP, TOK_TILES, NOPE + ROPE], F32, name="ks_stage%d" % b)
            for b in range(2)
        ]
        both = [P, TOK_TILES, 2, HALF_ROPE]
        by_sin = const.tile(both, F32, name="by_sin")
        by_cos = const.tile(both, F32, name="by_cos")
        rotated = const.tile(both, F32, name="rotated")

        def multiply_k_pe():
            nc.vector.tensor_tensor(
                out=by_sin[:], in0=kp[:], in1=sin_cos[:, 0].unsqueeze(2).to_broadcast(both),
                op=ALU.mult,
            )
            nc.vector.tensor_tensor(
                out=by_cos[:], in0=kp[:], in1=sin_cos[:, 1].unsqueeze(2).to_broadcast(both),
                op=ALU.mult,
            )

        def rotate_k_pe():
            nc.vector.tensor_tensor(
                out=rotated[:, :, 0, :], in0=by_cos[:, :, 0, :], in1=by_sin[:, :, 1, :],
                op=ALU.subtract,
            )
            nc.vector.tensor_tensor(
                out=rotated[:, :, 1, :], in0=by_sin[:, :, 0, :], in1=by_cos[:, :, 1, :],
                op=ALU.add,
            )

        def fill_rope(b, half):
            toks = slice(HALF_TILES * half, HALF_TILES * (half + 1))
            nc.vector.tensor_copy(
                out=ks_stage[b][:, :, toks, NOPE:],
                in_=rotated[:, toks, :, :]
                .rearrange("p i s j -> p i (s j)")
                .unsqueeze(1)
                .to_broadcast([P, GROUP, HALF_TILES, ROPE]),
            )

        gain = const.tile([P, PACK, P], F32, name="gain")

        def spread_gain():
            gain_ps = psum.tile([P, KVR], F32, tag="bank", name="gain_ps")
            nc.tensor.matmul(gain_ps[:], lhsT=ones[:], rhs=gain_row[:], start=True, stop=True)
            return gain_ps

        def keep_gain(gain_ps):
            nc.scalar.copy(out=gain[:], in_=gain_ps[:].rearrange("p (q t) -> p t q", t=PACK))

        def codes_and_scales(name, width):
            codes = keep.tile([P, width], U32, name=name + "_codes", align_bytes=64)
            scales = keep.tile([P, width], U8, name=name + "_scales", align_bytes=64)
            return codes, scales

        x_q = [codes_and_scales("x%d" % i, X_PASSES * P) for i in range(TOK_TILES)]
        wc_q = [codes_and_scales("wc%d" % g, KVR) for g in range(X_PASSES)]
        cn_q = [codes_and_scales("cn%d" % i, P) for i in range(TOK_TILES)]
        wv_q = [codes_and_scales("wv%d" % m, GROUP * VD) for m in range(GROUPS)]
        wk_q = [codes_and_scales("wk%d" % m, GROUP * NOPE) for m in range(GROUPS)]

        def quantise(grouped, pair):
            codes, scales = pair
            nc.vector.quantize_mx(
                out=codes[:].bitcast(FP8X4), scales=scales[:], in_=grouped
            )

        def mx(out, lhs, lhs_cols, rhs, rhs_cols, start, stop):
            nc.tensor.matmul_mx(
                out=out,
                lhsT=lhs[0][:, lhs_cols].bitcast(FP8X4),
                lhsT_scale=lhs[1][:, lhs_cols],
                rhs=rhs[0][:, rhs_cols].bitcast(FP8X4),
                rhs_scale=rhs[1][:, rhs_cols],
                start=start,
                stop=stop,
            )

        def leave_psum(n, share, out, in_):
            if n % share < share - 1:
                nc.scalar.copy(out=out, in_=in_)
            else:
                nc.vector.tensor_copy(out=out, in_=in_)

        x_grouped = {}
        cn_rows = {}
        cn_grouped = {}

        def transpose_x(i, banks=(0, 1)):
            words = x_rows(i).bitcast(F32)
            if banks[0] == 0:
                x_grouped[i] = work.tile(
                    [P, X_PASSES * P * PACK], BF16, tag="grouped", bufs=5, align_bytes=64,
                    name="x_grouped",
                )
            grouped_words = x_grouped[i][:].bitcast(F32)
            for bank in banks:
                xt = psum.tile([P, 4, P], F32, tag="bank", name="xt")
                for s in range(4):
                    first = 2 * P * (2 * bank + s // 2)
                    nc.tensor.transpose(
                        xt[:, s, :], words[:, first + s % 2 : first + 2 * P : 2], ident_f32[:]
                    )
                nc.scalar.copy(
                    out=grouped_words[:, 512 * bank : 512 * (bank + 1)].rearrange(
                        "p (g r u) -> p g r u", g=2, u=2
                    ),
                    in_=xt[:].rearrange("p (g u) r -> p g r u", u=2),
                )

        def quantise_x(i):
            quantise(x_grouped[i][:], x_q[i])

        acc_of = {}
        mean_sq_of = {}
        rms_of = {}
        inv_rms_of = {}

        def project(i):
            acc = psum.tile([P, KVR], F32, tag="bank", name="acc")
            for g in range(X_PASSES):
                mx(acc[:], x_q[i], slice(P * g, P * (g + 1)), wc_q[g], slice(0, KVR),
                   g == 0, g == X_PASSES - 1)
            squares = work.tile([P, KVR], BF16, tag="squares", name="squares")
            mean_sq = work.tile([P, 1], F32, tag="mean_sq", bufs=4, name="mean_sq")
            nc.scalar.activation(
                out=squares[:], in_=acc[:], func=ACT.Square,
                scale=1.0 / math.sqrt(KVR), accum_out=mean_sq[:],
            )
            acc_of[i] = acc
            mean_sq_of[i] = mean_sq

        def root(i):
            rms = work.tile([P, 1], F32, tag="rms", bufs=4, name="rms")
            nc.scalar.activation(out=rms[:], in_=mean_sq_of[i][:], func=ACT.Sqrt, bias=EPS)
            rms_of[i] = rms

        def invert_rms(i):
            inv_rms = work.tile([P, 1], F32, tag="inv_rms", bufs=4, name="inv_rms")
            nc.vector.reciprocal(out=inv_rms[:], in_=rms_of[i][:])
            inv_rms_of[i] = inv_rms

        def scale_cn(i):
            acc = acc_of[i]
            inv_rms = inv_rms_of[i]
            cn = work.tile([P, PACK, P], BF16, tag="cn", bufs=4, name="cn")
            nc.vector.scalar_tensor_tensor(
                out=cn[:],
                in0=acc[:].rearrange("p (q t) -> p t q", t=PACK),
                scalar=inv_rms[:, 0:1],
                in1=gain[:],
                op0=ALU.mult,
                op1=ALU.mult,
            )
            cn_rows[i] = cn

        def normalise(i):
            invert_rms(i)
            scale_cn(i)

        def transpose_cn(i):
            cn_t = psum.tile([P, PACK, P], BF16, tag="bank", name="cn_t")
            for t in range(PACK):
                nc.tensor.transpose(cn_t[:, t, :], cn_rows[i][:, t, :], ident_bf16[:])
            grouped = work.tile(
                [P, P, PACK], BF16, tag="cn_grouped", bufs=4, align_bytes=64, name="cn_grouped"
            )
            nc.scalar.copy(out=grouped[:], in_=cn_t[:].rearrange("p t r -> p r t"))
            cn_grouped[i] = grouped

        def quantise_cn(i):
            quantise(cn_grouped[i][:].rearrange("p r t -> p (r t)"), cn_q[i])

        def grouped_columns(width):
            grouped = work.tile(
                [P, X_PASSES * P * PACK], BF16, tag="grouped", bufs=5, align_bytes=64,
                name="w_grouped",
            )
            return grouped[:, 0 : width * PACK]

        def regroup_wc(g):
            flat = grouped_columns(KVR)
            dst = flat.rearrange("p (c i t) -> p c t i", i=RUN, t=PACK)
            src = wc_raw[g][:].rearrange("p t (c i) -> p c t i", i=RUN)
            middle = KVR // RUN // 2 if g > 0 else 0
            if middle:
                nc.scalar.copy(out=dst[:, 0:middle], in_=src[:, 0:middle])
            nc.vector.tensor_copy(out=dst[:, middle:], in_=src[:, middle:])
            return flat

        def regroup_wb(m, first, width, flat, part, on_scalar):
            w = m // 2
            head = GROUP * (m - wb_groups[w][0])
            heads = wb_raw[w][:].rearrange("p t (h f) -> p t h f", f=HEAD_COLS)
            dst = flat.rearrange("p (h c i t) -> p h c t i", h=GROUP, i=RUN, t=PACK)
            src = heads[:, :, head : head + GROUP, first : first + width].rearrange(
                "p t h (c i) -> p h c t i", i=RUN
            )
            if on_scalar:
                nc.scalar.copy(out=dst[:, part], in_=src[:, part])
            else:
                nc.vector.tensor_copy(out=dst[:, part], in_=src[:, part])

        v_stage_of = {}

        def v_tiles(m, half, share, tiles):
            if tiles[0] == 0:
                v_stage_of[m, half] = work.tile(
                    [P, GROUP, HALF_TILES, VD], F32, tag="v_stage", bufs=4, name="v_stage"
                )
            stage = v_stage_of[m, half]
            for s in tiles:
                i = HALF_TILES * half + s
                kv = psum.tile([P, GROUP * VD], F32, tag="bank", name="kv")
                mx(kv[:], cn_q[i], slice(0, P), wv_q[m], slice(0, GROUP * VD), True, True)
                leave_psum(
                    s, share, stage[:, :, s, :], kv[:].rearrange("p (h d) -> p h d", h=GROUP)
                )
            if tiles[-1] < HALF_TILES - 1:
                return
            nc.sync.dma_start(
                out=v_view[:, GROUP * m : GROUP * (m + 1),
                           HALF_TILES * half : HALF_TILES * (half + 1), :],
                in_=stage[:],
            )

        def v_half(m, half, share):
            v_tiles(m, half, share, range(HALF_TILES))

        def v_pair(m, pair):
            stage = work.tile([P, PAIR, TOK_TILES, VD], F32, tag="v_stage", bufs=4,
                              name="v_stage")
            width = PAIR * VD
            for b in range(TOK_TILES // 2):
                kv = psum.tile([P, 2, width], F32, tag="bank", name="kv")
                for s in range(2):
                    mx(kv[:, s, :], cn_q[2 * b + s], slice(0, P), wv_q[m],
                       slice(width * pair, width * (pair + 1)), True, True)
                leave_psum(
                    b, 2,
                    stage[:, :, 2 * b : 2 * b + 2, :].rearrange("p h i d -> p i h d"),
                    kv[:].rearrange("p i (h d) -> p i h d", h=PAIR),
                )
            head = GROUP * m + PAIR * pair
            nc.sync.dma_start(out=v_view[:, head : head + PAIR, :, :], in_=stage[:])

        def k_tiles(m, first, tiles, share):
            stage = ks_stage[m % 2]
            for b in range(tiles // 2):
                kk = psum.tile([P, 2, GROUP * NOPE], F32, tag="bank", name="kk")
                at = first + 2 * b
                for s in range(2):
                    mx(kk[:, s, :], cn_q[at + s], slice(0, P), wk_q[m],
                       slice(0, GROUP * NOPE), True, True)
                leave_psum(
                    b, share,
                    stage[:, :, at : at + 2, 0:NOPE].rearrange("p h i d -> p i h d"),
                    kk[:].rearrange("p i (h d) -> p i h d", h=GROUP),
                )
            nc.sync.dma_start(
                out=ks_view[:, GROUP * m : GROUP * (m + 1), first : first + tiles, :],
                in_=stage[:, :, first : first + tiles, :],
            )

        flat_of = {}

        def regroup_v(m, part=slice(0, GROUP), on_scalar=False):
            if (m, 0) not in flat_of:
                flat_of[m, 0] = grouped_columns(GROUP * VD)
            regroup_wb(m, NOPE, VD, flat_of[m, 0], part, on_scalar)

        def regroup_k(m, part=slice(0, GROUP), on_scalar=False):
            if (m, 1) not in flat_of:
                flat_of[m, 1] = grouped_columns(GROUP * NOPE)
            regroup_wb(m, 0, NOPE, flat_of[m, 1], part, on_scalar)

        def quantise_v(m):
            quantise(flat_of[m, 0], wv_q[m])

        def quantise_k(m):
            quantise(flat_of[m, 1], wk_q[m])

        def unit(u, half, share):
            kind, m = u
            if kind == "v":
                v_half(m, half, share)
            else:
                k_tiles(m, HALF_TILES * half, HALF_TILES, share)

        def regroup_unit(u):
            kind, m = u
            if kind == "v":
                regroup_v(m)
            else:
                regroup_k(m)

        def quantise_unit(u):
            kind, m = u
            if kind == "v":
                quantise_v(m)
            else:
                quantise_k(m)

        flats = {}
        for g in range(X_PASSES):
            flats[g] = regroup_wc(g)
            if g > 0:
                quantise(flats[g - 1], wc_q[g - 1])
        quantise(flats[X_PASSES - 1], wc_q[X_PASSES - 1])
        multiply_k_pe()
        gain_ps = spread_gain()
        transpose_x(0)
        transpose_x(1)
        transpose_x(2)
        transpose_x(3)
        keep_gain(gain_ps)
        quantise_x(0)
        rotate_k_pe()
        quantise_x(1)
        quantise_x(2)
        fill_rope(0, 0)
        quantise_x(3)
        project(0)
        root(0)
        project(1)
        root(1)
        project(2)
        root(2)
        project(3)
        root(3)
        invert_rms(0)
        scale_cn(0)
        regroup_k(0)
        quantise_k(0)
        normalise(1)
        normalise(2)
        normalise(3)
        transpose_cn(0)
        transpose_cn(1)
        transpose_cn(2)
        transpose_cn(3)
        quantise_cn(0)
        quantise_cn(1)
        quantise_cn(2)
        quantise_cn(3)
        unit(("k", 0), 0, 9)
        regroup_k(1)
        fill_rope(1, 0)
        quantise_k(1)
        transpose_x(4)
        unit(("k", 1), 0, 9)
        regroup_v(0)
        transpose_x(5)
        quantise_v(0)
        quantise_x(4)
        unit(("v", 0), 0, 2)
        regroup_k(2)
        quantise_k(2)
        transpose_x(6)
        transpose_x(7)
        unit(("k", 2), 0, 9)
        quantise_x(5)
        regroup_k(3)
        quantise_k(3)
        project(4)
        root(4)
        project(5)
        root(5)
        unit(("k", 3), 0, 9)
        quantise_x(6)
        regroup_v(1)
        quantise_x(7)
        normalise(4)
        normalise(5)
        quantise_v(1)
        project(6)
        root(6)
        project(7)
        root(7)
        normalise(6)
        unit(("v", 1), 0, 2)
        normalise(7)
        transpose_cn(4)
        transpose_cn(5)
        quantise_cn(4)
        quantise_cn(5)
        transpose_cn(6)
        transpose_cn(7)
        fill_rope(0, 1)
        quantise_cn(6)
        quantise_cn(7)
        unit(("k", 0), 1, 2)
        unit(("v", 0), 1, 2)
        fill_rope(1, 1)
        unit(("k", 1), 1, 2)
        regroup_v(2)
        unit(("k", 2), 1, 2)
        quantise_v(2)
        unit(("v", 1), 1, 2)
        regroup_v(3)
        unit(("k", 3), 1, 2)
        quantise_v(3)
        v_pair(2, 0)
        v_pair(2, 1)
        v_pair(3, 0)
        v_pair(3, 1)
